import numpy as np
import ml_dtypes


def mxq(x, axis, fmt="e4m3"):
    dtype, down = {"e4m3": (ml_dtypes.float8_e4m3fn, 7), "e5m2": (ml_dtypes.float8_e5m2, 14)}[fmt]
    v = np.moveaxis(np.asarray(x, np.float32).astype(ml_dtypes.bfloat16).astype(np.float64), axis, -1)
    blocks = v.reshape(v.shape[:-1] + (-1, 32))
    amax = np.abs(blocks).max(-1, keepdims=True)
    byte = np.maximum(np.where(amax > 0, np.frexp(amax)[1] - 1 + 127, 0) - down, 1)
    scale = np.exp2(byte - 127.0)
    codes = (blocks / scale).astype(np.float32).astype(dtype).astype(np.float64)
    return np.moveaxis((codes * scale).reshape(v.shape), -1, axis)


WIDE = False


def mx_kscale(k):
    if not WIDE:
        return np.ones(k)
    levels = np.array([10, -10, 5, -5, 0])
    a = np.random.permutation(np.resize(levels, k // 512 * 4)).reshape(k // 512, 4)
    idx = np.arange(k)
    return np.exp2(a[idx // 512, idx % 128 // 32])


BF16 = ml_dtypes.bfloat16


def bf(x):
    return np.asarray(x, np.float32).astype(BF16)


def f64(x):
    return np.asarray(x).astype(np.float64)


B, IN_F, N_HID = 4096, 768, 256
HEAD = N_HID + IN_F


def sigmoid(v):
    return 1.0 / (1.0 + np.exp(-v))


def setup_inputs():
    s = mx_kscale(HEAD)
    scale = 1.0 / np.sqrt(HEAD)
    raw = np.abs(np.random.randint(-1, 2, (IN_F, N_HID))).astype(np.float64)
    rec = (np.random.random((N_HID, N_HID)) < 0.9).astype(np.float64)
    mask = np.concatenate([raw, rec], axis=0).T

    def w():
        return bf(np.random.standard_normal((N_HID, HEAD)) * scale / s[None, :])

    def b():
        return bf(np.random.standard_normal(N_HID) * 0.3)

    return {
        "x": bf(np.random.standard_normal((B, IN_F)) * s[None, :IN_F]),
        "hidden": bf(np.random.standard_normal((B, N_HID)) * s[None, IN_F:]),
        "mask": bf(mask),
        "Wg": w(), "bg": b(),
        "Wh": w(), "bh": b(),
        "Wfg": w(), "bfg": b(),
        "Wfh": w(), "bfh": b(),
        "Wp": w(), "bp": b(),
    }


def reference(x, hidden, mask, Wg, bg, Wh, bh, Wfg, bfg, Wfh, bfh, Wp, bp):
    xc = np.concatenate([f64(x), f64(hidden)], axis=1)
    W_all = np.stack([f64(Wg), f64(Wh), f64(Wfg), f64(Wfh), f64(Wp)]) * f64(mask)[None]
    b_all = np.stack([f64(bg), f64(bh), f64(bfg), f64(bfh), f64(bp)])
    outs = (mxq(xc, 1, "e4m3") @ mxq(W_all, 2, "e4m3").transpose(0, 2, 1)) + b_all[:, None, :]
    g_out, h_out, fg_out, fh_out, p_out = outs
    g = np.tanh(g_out)
    h = np.tanh(h_out)
    gate = sigmoid(fg_out + fh_out)
    new_hidden = g * (1.0 - gate) + gate * h
    y_pred = p_out + new_hidden
    return (y_pred, new_hidden)

@@ -1,0 +1,234 @@
+from contextlib import ExitStack
+
+import concourse.mybir as mybir
+from concourse.masks import make_identity
+
+F32 = mybir.dt.float32
+BF16 = mybir.dt.bfloat16
+U32 = mybir.dt.uint32
+U8 = mybir.dt.uint8
+FP8X4 = mybir.dt.float8_e4m3fn_x4
+ALU = mybir.AluOpType
+ACT = mybir.ActivationFunctionType
+
+P = 128
+B, IN_F, N_HID = 4096, 768, 256
+K = IN_F + N_HID
+SB = 512
+JT = SB // P
+NSB = B // SB
+FLOPS = 2 * B * K * 5 * N_HID
+
+
+def tile_ncpliquidcell_t_kernel(
+    tc, x, hidden, mask, Wg, bg, Wh, bh, Wfg, bfg, Wfh, bfh, Wp, bp, out_0, out_1
+):
+    nc = tc.nc
+    weights = [Wg, Wh, Wfg, Wfh, Wp]
+    with ExitStack() as ctx:
+        const = ctx.enter_context(tc.tile_pool(name="const", bufs=1))
+        wraw = ctx.enter_context(tc.tile_pool(name="wraw", bufs=5))
+        wgr = ctx.enter_context(tc.tile_pool(name="wgr", bufs=2))
+        xin = ctx.enter_context(tc.tile_pool(name="xin", bufs=NSB))
+        xgr = ctx.enter_context(tc.tile_pool(name="xgr", bufs=2))
+        xq = ctx.enter_context(tc.tile_pool(name="xq", bufs=3))
+        act = ctx.enter_context(tc.tile_pool(name="act", bufs=2))
+        ep = ctx.enter_context(tc.tile_pool(name="ep", bufs=2))
+        outp = ctx.enter_context(tc.tile_pool(name="outp", bufs=3))
+        tr = ctx.enter_context(tc.psum_pool(name="tr", bufs=4))
+        mx = ctx.enter_context(tc.psum_pool(name="mx", bufs=4))
+
+        warm = const.tile([P, 1], F32)
+        nc.vector.memset(warm[:], 0.0)
+        warm2 = const.tile([P, 1], F32)
+        nc.scalar.activation(out=warm2[:], in_=warm[:], func=ACT.Tanh)
+        ident = const.tile([P, P], F32)
+        make_identity(nc, ident[:])
+        zt_bf = const.tile([P, P], BF16)
+        nc.vector.memset(zt_bf[:], 0.0)
+        zb_bf = const.tile([P, N_HID], BF16)
+        nc.vector.memset(zb_bf[:], 0.0)
+        ones_bf = const.tile([P, P], BF16)
+        nc.vector.memset(ones_bf[:], 1.0)
+
+        mask_sb = const.tile([P, 2, K], BF16)
+        w_sb = [wraw.tile([P, 2, K], BF16, name="w%d" % w, tag="w") for w in range(5)]
+        x_sb = [xin.tile([P, JT, IN_F], BF16, name="x%d" % s, tag="x") for s in range(NSB)]
+        h_sb = [xin.tile([P, JT, N_HID], BF16, name="h%d" % s, tag="h") for s in range(NSB)]
+
+        def load_w(w):
+            nc.sync.dma_start(out=w_sb[w][:], in_=weights[w].rearrange("(h p) k -> p h k", p=P))
+
+        def load_x(s):
+            rows = slice(SB * s, SB * (s + 1))
+            nc.sync.dma_start(out=x_sb[s][:], in_=x[rows, :].rearrange("(p j) k -> p j k", j=JT))
+            nc.sync.dma_start(out=h_sb[s][:], in_=hidden[rows, :].rearrange("(p j) k -> p j k", j=JT))
+
+        nc.sync.dma_start(out=mask_sb[:], in_=mask.rearrange("(h p) k -> p h k", p=P))
+        load_w(0)
+        load_x(0)
+        for w in range(1, 5):
+            load_w(w)
+        for s in range(1, NSB):
+            load_x(s)
+        for i, b in enumerate([bg, bh, bfg, bfh]):
+            nc.scalar.dma_start(out=zt_bf[2 * i : 2 * i + 2, :], in_=b.rearrange("(r c) -> r c", r=2))
+        nc.scalar.dma_start(out=zb_bf[0:1, :], in_=bp.rearrange("(o c) -> o c", o=1))
+
+        zt = const.tile([P, P], F32)
+        nc.vector.tensor_copy(out=zt[:], in_=zt_bf[:])
+        bt = tr.tile([P, 512], F32, tag="tr")
+        nc.tensor.transpose(bt[:, 0:P], zt[:], ident[:])
+        bias_sb = const.tile([P, 8], F32)
+        nc.vector.tensor_copy(out=bias_sb[:], in_=bt[:, 0:8])
+        bf_sum = const.tile([P, 2], F32)
+        nc.vector.tensor_tensor(out=bf_sum[:], in0=bias_sb[:, 4:6], in1=bias_sb[:, 6:8], op=ALU.add)
+        bf_half = const.tile([P, 2], F32)
+        nc.vector.tensor_scalar_mul(out=bf_half[:], in0=bf_sum[:], scalar1=0.5)
+        bb = tr.tile([P, 512], F32, tag="tr")
+        nc.tensor.matmul(out=bb[:, 0:N_HID], lhsT=ones_bf[:], rhs=zb_bf[:], start=True, stop=True)
+        bp_bc = const.tile([P, 2, N_HID], F32)
+        for r in range(2):
+            nc.vector.tensor_copy(out=bp_bc[:, r, :], in_=bb[:, 0:N_HID])
+
+        wc = [const.tile([P, 2, N_HID], U32, name="wc%d" % w, align_bytes=64) for w in range(5)]
+        ws = [const.tile([P, 2, N_HID], U8, name="ws%d" % w, align_bytes=64) for w in range(5)]
+
+        def prep_w(w):
+            wg = wgr.tile([P, 2, N_HID, 2], F32, tag="wg", align_bytes=64)
+            for hf in range(2):
+                nc.vector.tensor_tensor(
+                    out=w_sb[w][:, hf, :], in0=w_sb[w][:, hf, :], in1=mask_sb[:, hf, :], op=ALU.mult
+                )
+                wt = tr.tile([P, 512], F32, tag="tr")
+                ww = w_sb[w][:, hf, :].bitcast(F32)
+                for b in range(4):
+                    nc.tensor.transpose(wt[:, P * b : P * (b + 1)], ww[:, P * b : P * (b + 1)], ident[:])
+                nc.scalar.copy(
+                    out=wg[:, :, P * hf : P * (hf + 1), :],
+                    in_=wt[:].rearrange("q (g u c) -> q g c u", g=2, u=2),
+                )
+            nc.vector.quantize_mx(
+                out=wc[w][:].rearrange("q g c -> q (g c)").bitcast(FP8X4),
+                scales=ws[w][:].rearrange("q g c -> q (g c)"),
+                in_=wg[:].rearrange("q g c u -> q (g c u)").bitcast(BF16),
+            )
+
+        xc = {}
+        xs = {}
+
+        def stage_t(s):
+            xg = xgr.tile([P, 2, SB, 2], F32, tag="xg", align_bytes=64)
+            for j in range(JT):
+                xt = tr.tile([P, 512], F32, tag="tr")
+                xw = x_sb[s][:, j, :].bitcast(F32)
+                hw = h_sb[s][:, j, :].bitcast(F32)
+                for b in range(3):
+                    nc.tensor.transpose(xt[:, P * b : P * (b + 1)], xw[:, P * b : P * (b + 1)], ident[:])
+                nc.tensor.transpose(xt[:, 3 * P : 4 * P], hw, ident[:])
+                nc.scalar.copy(
+                    out=xg[:, :, P * j : P * (j + 1), :],
+                    in_=xt[:].rearrange("q (g u c) -> q g c u", g=2, u=2),
+                )
+            codes = xq.tile([P, 2, SB], U32, tag="xc", align_bytes=64)
+            scales = xq.tile([P, 2, SB], U8, tag="xs", align_bytes=64)
+            nc.vector.quantize_mx(
+                out=codes[:].rearrange("q g c -> q (g c)").bitcast(FP8X4),
+                scales=scales[:].rearrange("q g c -> q (g c)"),
+                in_=xg[:].rearrange("q g c u -> q (g c u)").bitcast(BF16),
+            )
+            xc[s] = codes
+            xs[s] = scales
+
+        keep = {}
+
+        def stage_m(s):
+            codes = xc[s]
+            scales = xs[s]
+            g_t = act.tile([P, 2, SB], F32, tag="g")
+            h_t = act.tile([P, 2, SB], F32, tag="h")
+            t_t = act.tile([P, 2, SB], F32, tag="t")
+            d_t = ep.tile([P, 2, SB], F32, tag="d")
+            nh = ep.tile([P, 2, SB], F32, tag="nh")
+            pb = outp.tile([P, JT, N_HID], F32, tag="pb")
+
+            def layer(wlist, hf, dst, bias, scale):
+                acc = mx.tile([P, 512], F32, tag="mx")
+                cols = slice(P * hf, P * (hf + 1))
+                n = 2 * len(wlist)
+                i = 0
+                for w in wlist:
+                    for g in range(2):
+                        nc.tensor.matmul_mx(
+                            out=acc[:],
+                            lhsT=wc[w][:, g, cols].bitcast(FP8X4),
+                            lhsT_scale=ws[w][:, g, cols],
+                            rhs=codes[:, g, :].bitcast(FP8X4),
+                            rhs_scale=scales[:, g, :],
+                            start=(i == 0),
+                            stop=(i == n - 1),
+                        )
+                        i += 1
+                nc.scalar.activation(out=dst[:, hf, :], in_=acc[:], func=ACT.Tanh, bias=bias, scale=scale)
+
+            for hf in range(2):
+                layer([0], hf, g_t, bias_sb[:, hf : hf + 1], 1.0)
+                layer([1], hf, h_t, bias_sb[:, 2 + hf : 3 + hf], 1.0)
+                layer([2, 3], hf, t_t, bf_half[:, hf : hf + 1], 0.5)
+                nc.vector.tensor_tensor(out=d_t[:, hf, :], in0=h_t[:, hf, :], in1=g_t[:, hf, :], op=ALU.subtract)
+                nc.vector.scalar_tensor_tensor(
+                    out=d_t[:, hf, :], in0=t_t[:, hf, :], scalar=1.0, in1=d_t[:, hf, :], op0=ALU.add, op1=ALU.mult
+                )
+                nc.vector.scalar_tensor_tensor(
+                    out=nh[:, hf, :], in0=d_t[:, hf, :], scalar=0.5, in1=g_t[:, hf, :], op0=ALU.mult, op1=ALU.add
+                )
+            for jp in range(2):
+                acc = mx.tile([P, 512], F32, tag="mx")
+                for jj in range(2):
+                    j = 2 * jp + jj
+                    cols = slice(P * j, P * (j + 1))
+                    for g in range(2):
+                        nc.tensor.matmul_mx(
+                            out=acc[:, N_HID * jj : N_HID * (jj + 1)],
+                            lhsT=codes[:, g, cols].bitcast(FP8X4),
+                            lhsT_scale=scales[:, g, cols],
+                            rhs=wc[4][:, g, :].bitcast(FP8X4),
+                            rhs_scale=ws[4][:, g, :],
+                            start=(g == 0),
+                            stop=(g == 1),
+                        )
+                nc.vector.tensor_tensor(
+                    out=pb[:, 2 * jp : 2 * jp + 2, :].rearrange("p a f -> p (a f)"),
+                    in0=acc[:],
+                    in1=bp_bc[:].rearrange("p a f -> p (a f)"),
+                    op=ALU.add,
+                )
+            keep[s] = (nh, pb)
+
+        def stage_n(s):
+            nh, pb = keep[s]
+            rows = slice(SB * s, SB * (s + 1))
+            nht = outp.tile([P, JT, N_HID], F32, tag="nht")
+            y_t = outp.tile([P, JT, N_HID], F32, tag="y")
+            for jp in range(2):
+                nt = tr.tile([P, 512], F32, tag="tr")
+                for jj in range(2):
+                    j = 2 * jp + jj
+                    for hf in range(2):
+                        o = N_HID * jj + P * hf
+                        nc.tensor.transpose(nt[:, o : o + P], nh[:, hf, P * j : P * (j + 1)], ident[:])
+                nc.scalar.copy(out=nht[:, 2 * jp : 2 * jp + 2, :].rearrange("p a f -> p (a f)"), in_=nt[:])
+            nc.vector.tensor_tensor(out=y_t[:], in0=nht[:], in1=pb[:], op=ALU.add)
+            nc.sync.dma_start(out=out_1[rows, :].rearrange("(p j) f -> p j f", j=JT), in_=nht[:])
+            nc.sync.dma_start(out=out_0[rows, :].rearrange("(p j) f -> p j f", j=JT), in_=y_t[:])
+
+        prep_w(0)
+        stage_t(0)
+        for w in range(1, 5):
+            prep_w(w)
+        stage_t(1)
+        for s in range(NSB):
+            stage_m(s)
+            if s + 2 < NSB:
+                stage_t(s + 2)
+            stage_n(s)

@@ -37,6 +37,7 @@ def tile_ncpliquidcell_t_kernel(
         outp = ctx.enter_context(tc.tile_pool(name="outp", bufs=3))
         tr = ctx.enter_context(tc.psum_pool(name="tr", bufs=4))
         mx = ctx.enter_context(tc.psum_pool(name="mx", bufs=4))
+        ctx.enter_context(tc.manual_schedule())
 
         warm = const.tile([P, 1], F32)
         nc.vector.memset(warm[:], 0.0)
@@ -56,6 +57,9 @@ def tile_ncpliquidcell_t_kernel(
         x_sb = [xin.tile([P, JT, IN_F], BF16, name="x%d" % s, tag="x") for s in range(NSB)]
         h_sb = [xin.tile([P, JT, N_HID], BF16, name="h%d" % s, tag="h") for s in range(NSB)]
 
+        def load_m():
+            nc.sync.dma_start(out=mask_sb[:], in_=mask.rearrange("(h p) k -> p h k", p=P))
+
         def load_w(w):
             nc.sync.dma_start(out=w_sb[w][:], in_=weights[w].rearrange("(h p) k -> p h k", p=P))
 
@@ -64,13 +68,20 @@ def tile_ncpliquidcell_t_kernel(
             nc.sync.dma_start(out=x_sb[s][:], in_=x[rows, :].rearrange("(p j) k -> p j k", j=JT))
             nc.sync.dma_start(out=h_sb[s][:], in_=hidden[rows, :].rearrange("(p j) k -> p j k", j=JT))
 
-        nc.sync.dma_start(out=mask_sb[:], in_=mask.rearrange("(h p) k -> p h k", p=P))
-        load_w(0)
         load_x(0)
-        for w in range(1, 5):
-            load_w(w)
-        for s in range(1, NSB):
-            load_x(s)
+        load_m()
+        load_w(0)
+        load_w(1)
+        load_w(2)
+        load_w(3)
+        load_w(4)
+        load_x(1)
+        load_x(2)
+        load_x(3)
+        load_x(4)
+        load_x(5)
+        load_x(6)
+        load_x(7)
         for i, b in enumerate([bg, bh, bfg, bfh]):
             nc.scalar.dma_start(out=zt_bf[2 * i : 2 * i + 2, :], in_=b.rearrange("(r c) -> r c", r=2))
         nc.scalar.dma_start(out=zb_bf[0:1, :], in_=bp.rearrange("(o c) -> o c", o=1))
@@ -93,142 +104,511 @@ def tile_ncpliquidcell_t_kernel(
 
         wc = [const.tile([P, 2, N_HID], U32, name="wc%d" % w, align_bytes=64) for w in range(5)]
         ws = [const.tile([P, 2, N_HID], U8, name="ws%d" % w, align_bytes=64) for w in range(5)]
+        t = {}
 
-        def prep_w(w):
-            wg = wgr.tile([P, 2, N_HID, 2], F32, tag="wg", align_bytes=64)
-            for hf in range(2):
-                nc.vector.tensor_tensor(
-                    out=w_sb[w][:, hf, :], in0=w_sb[w][:, hf, :], in1=mask_sb[:, hf, :], op=ALU.mult
-                )
-                wt = tr.tile([P, 512], F32, tag="tr")
-                ww = w_sb[w][:, hf, :].bitcast(F32)
-                for b in range(4):
-                    nc.tensor.transpose(wt[:, P * b : P * (b + 1)], ww[:, P * b : P * (b + 1)], ident[:])
-                nc.scalar.copy(
-                    out=wg[:, :, P * hf : P * (hf + 1), :],
-                    in_=wt[:].rearrange("q (g u c) -> q g c u", g=2, u=2),
-                )
+        def copy_on(eng, out, in_):
+            if eng == "S":
+                nc.scalar.copy(out=out, in_=in_)
+            else:
+                nc.vector.tensor_copy(out=out, in_=in_)
+
+        def mm(w, hf):
+            nc.vector.tensor_tensor(out=w_sb[w][:, hf, :], in0=w_sb[w][:, hf, :], in1=mask_sb[:, hf, :], op=ALU.mult)
+
+        def wt(w, hf):
+            bank = tr.tile([P, 512], F32, tag="tr", name="wt")
+            t["wt", w, hf] = bank
+            ww = w_sb[w][:, hf, :].bitcast(F32)
+            for b in range(4):
+                nc.tensor.transpose(bank[:, P * b : P * (b + 1)], ww[:, P * b : P * (b + 1)], ident[:])
+
+        def wcp(w, hf, eng):
+            if ("wg", w) not in t:
+                t["wg", w] = wgr.tile([P, 2, N_HID, 2], F32, tag="wg", name="wg", align_bytes=64)
+            copy_on(
+                eng,
+                t["wg", w][:, :, P * hf : P * (hf + 1), :],
+                t["wt", w, hf][:].rearrange("q (g u c) -> q g c u", g=2, u=2),
+            )
+
+        def wq(w):
             nc.vector.quantize_mx(
                 out=wc[w][:].rearrange("q g c -> q (g c)").bitcast(FP8X4),
                 scales=ws[w][:].rearrange("q g c -> q (g c)"),
-                in_=wg[:].rearrange("q g c u -> q (g c u)").bitcast(BF16),
+                in_=t["wg", w][:].rearrange("q g c u -> q (g c u)").bitcast(BF16),
             )
 
-        xc = {}
-        xs = {}
+        def xt(s, j):
+            bank = tr.tile([P, 512], F32, tag="tr", name="xt")
+            t["xt", s, j] = bank
+            xw = x_sb[s][:, j, :].bitcast(F32)
+            for b in range(3):
+                nc.tensor.transpose(bank[:, P * b : P * (b + 1)], xw[:, P * b : P * (b + 1)], ident[:])
+            nc.tensor.transpose(bank[:, 3 * P : 4 * P], h_sb[s][:, j, :].bitcast(F32), ident[:])
 
-        def stage_t(s):
-            xg = xgr.tile([P, 2, SB, 2], F32, tag="xg", align_bytes=64)
-            for j in range(JT):
-                xt = tr.tile([P, 512], F32, tag="tr")
-                xw = x_sb[s][:, j, :].bitcast(F32)
-                hw = h_sb[s][:, j, :].bitcast(F32)
-                for b in range(3):
-                    nc.tensor.transpose(xt[:, P * b : P * (b + 1)], xw[:, P * b : P * (b + 1)], ident[:])
-                nc.tensor.transpose(xt[:, 3 * P : 4 * P], hw, ident[:])
-                nc.scalar.copy(
-                    out=xg[:, :, P * j : P * (j + 1), :],
-                    in_=xt[:].rearrange("q (g u c) -> q g c u", g=2, u=2),
-                )
-            codes = xq.tile([P, 2, SB], U32, tag="xc", align_bytes=64)
-            scales = xq.tile([P, 2, SB], U8, tag="xs", align_bytes=64)
+        def xcp(s, j, eng):
+            if ("xg", s) not in t:
+                t["xg", s] = xgr.tile([P, 2, SB, 2], F32, tag="xg", name="xg", align_bytes=64)
+            copy_on(
+                eng,
+                t["xg", s][:, :, P * j : P * (j + 1), :],
+                t["xt", s, j][:].rearrange("q (g u c) -> q g c u", g=2, u=2),
+            )
+
+        def xqz(s):
+            t["xc", s] = xq.tile([P, 2, SB], U32, tag="xc", name="xc", align_bytes=64)
+            t["xs", s] = xq.tile([P, 2, SB], U8, tag="xs", name="xs", align_bytes=64)
             nc.vector.quantize_mx(
-                out=codes[:].rearrange("q g c -> q (g c)").bitcast(FP8X4),
-                scales=scales[:].rearrange("q g c -> q (g c)"),
-                in_=xg[:].rearrange("q g c u -> q (g c u)").bitcast(BF16),
+                out=t["xc", s][:].rearrange("q g c -> q (g c)").bitcast(FP8X4),
+                scales=t["xs", s][:].rearrange("q g c -> q (g c)"),
+                in_=t["xg", s][:].rearrange("q g c u -> q (g c u)").bitcast(BF16),
             )
-            xc[s] = codes
-            xs[s] = scales
 
-        keep = {}
+        layers = {"g": [0], "h": [1], "f": [2, 3]}
 
-        def stage_m(s):
-            codes = xc[s]
-            scales = xs[s]
-            g_t = act.tile([P, 2, SB], F32, tag="g")
-            h_t = act.tile([P, 2, SB], F32, tag="h")
-            t_t = act.tile([P, 2, SB], F32, tag="t")
-            d_t = ep.tile([P, 2, SB], F32, tag="d")
-            nh = ep.tile([P, 2, SB], F32, tag="nh")
-            pb = outp.tile([P, JT, N_HID], F32, tag="pb")
+        def mxl(s, lay, hf):
+            acc = mx.tile([P, 512], F32, tag="mx", name="acc")
+            t["acc", s, lay, hf] = acc
+            cols = slice(P * hf, P * (hf + 1))
+            wlist = layers[lay]
+            n = 2 * len(wlist)
+            i = 0
+            for w in wlist:
+                for g in range(2):
+                    nc.tensor.matmul_mx(
+                        out=acc[:],
+                        lhsT=wc[w][:, g, cols].bitcast(FP8X4),
+                        lhsT_scale=ws[w][:, g, cols],
+                        rhs=t["xc", s][:, g, :].bitcast(FP8X4),
+                        rhs_scale=t["xs", s][:, g, :],
+                        start=(i == 0),
+                        stop=(i == n - 1),
+                    )
+                    i += 1
 
-            def layer(wlist, hf, dst, bias, scale):
-                acc = mx.tile([P, 512], F32, tag="mx")
-                cols = slice(P * hf, P * (hf + 1))
-                n = 2 * len(wlist)
-                i = 0
-                for w in wlist:
-                    for g in range(2):
-                        nc.tensor.matmul_mx(
-                            out=acc[:],
-                            lhsT=wc[w][:, g, cols].bitcast(FP8X4),
-                            lhsT_scale=ws[w][:, g, cols],
-                            rhs=codes[:, g, :].bitcast(FP8X4),
-                            rhs_scale=scales[:, g, :],
-                            start=(i == 0),
-                            stop=(i == n - 1),
-                        )
-                        i += 1
-                nc.scalar.activation(out=dst[:, hf, :], in_=acc[:], func=ACT.Tanh, bias=bias, scale=scale)
+        def actl(s, lay, hf):
+            if (lay, s) not in t:
+                t[lay, s] = act.tile([P, 2, SB], F32, tag=lay, name="a" + lay)
+            if lay == "g":
+                bias, scale = bias_sb[:, hf : hf + 1], 1.0
+            elif lay == "h":
+                bias, scale = bias_sb[:, 2 + hf : 3 + hf], 1.0
+            else:
+                bias, scale = bf_half[:, hf : hf + 1], 0.5
+            nc.scalar.activation(out=t[lay, s][:, hf, :], in_=t["acc", s, lay, hf][:], func=ACT.Tanh, bias=bias, scale=scale)
 
-            for hf in range(2):
-                layer([0], hf, g_t, bias_sb[:, hf : hf + 1], 1.0)
-                layer([1], hf, h_t, bias_sb[:, 2 + hf : 3 + hf], 1.0)
-                layer([2, 3], hf, t_t, bf_half[:, hf : hf + 1], 0.5)
-                nc.vector.tensor_tensor(out=d_t[:, hf, :], in0=h_t[:, hf, :], in1=g_t[:, hf, :], op=ALU.subtract)
-                nc.vector.scalar_tensor_tensor(
-                    out=d_t[:, hf, :], in0=t_t[:, hf, :], scalar=1.0, in1=d_t[:, hf, :], op0=ALU.add, op1=ALU.mult
-                )
-                nc.vector.scalar_tensor_tensor(
-                    out=nh[:, hf, :], in0=d_t[:, hf, :], scalar=0.5, in1=g_t[:, hf, :], op0=ALU.mult, op1=ALU.add
-                )
-            for jp in range(2):
-                acc = mx.tile([P, 512], F32, tag="mx")
-                for jj in range(2):
-                    j = 2 * jp + jj
-                    cols = slice(P * j, P * (j + 1))
-                    for g in range(2):
-                        nc.tensor.matmul_mx(
-                            out=acc[:, N_HID * jj : N_HID * (jj + 1)],
-                            lhsT=codes[:, g, cols].bitcast(FP8X4),
-                            lhsT_scale=scales[:, g, cols],
-                            rhs=wc[4][:, g, :].bitcast(FP8X4),
-                            rhs_scale=ws[4][:, g, :],
-                            start=(g == 0),
-                            stop=(g == 1),
-                        )
-                nc.vector.tensor_tensor(
-                    out=pb[:, 2 * jp : 2 * jp + 2, :].rearrange("p a f -> p (a f)"),
-                    in0=acc[:],
-                    in1=bp_bc[:].rearrange("p a f -> p (a f)"),
-                    op=ALU.add,
-                )
-            keep[s] = (nh, pb)
+        def mxp(s, jp):
+            acc = mx.tile([P, 512], F32, tag="mx", name="accp")
+            t["accp", s, jp] = acc
+            for jj in range(2):
+                cols = slice(P * (2 * jp + jj), P * (2 * jp + jj + 1))
+                for g in range(2):
+                    nc.tensor.matmul_mx(
+                        out=acc[:, N_HID * jj : N_HID * (jj + 1)],
+                        lhsT=t["xc", s][:, g, cols].bitcast(FP8X4),
+                        lhsT_scale=t["xs", s][:, g, cols],
+                        rhs=wc[4][:, g, :].bitcast(FP8X4),
+                        rhs_scale=ws[4][:, g, :],
+                        start=(g == 0),
+                        stop=(g == 1),
+                    )
 
-        def stage_n(s):
-            nh, pb = keep[s]
-            rows = slice(SB * s, SB * (s + 1))
-            nht = outp.tile([P, JT, N_HID], F32, tag="nht")
-            y_t = outp.tile([P, JT, N_HID], F32, tag="y")
-            for jp in range(2):
-                nt = tr.tile([P, 512], F32, tag="tr")
-                for jj in range(2):
-                    j = 2 * jp + jj
-                    for hf in range(2):
-                        o = N_HID * jj + P * hf
-                        nc.tensor.transpose(nt[:, o : o + P], nh[:, hf, P * j : P * (j + 1)], ident[:])
-                nc.scalar.copy(out=nht[:, 2 * jp : 2 * jp + 2, :].rearrange("p a f -> p (a f)"), in_=nt[:])
-            nc.vector.tensor_tensor(out=y_t[:], in0=nht[:], in1=pb[:], op=ALU.add)
-            nc.sync.dma_start(out=out_1[rows, :].rearrange("(p j) f -> p j f", j=JT), in_=nht[:])
-            nc.sync.dma_start(out=out_0[rows, :].rearrange("(p j) f -> p j f", j=JT), in_=y_t[:])
+        def half(tile_, jp):
+            return tile_[:, 2 * jp : 2 * jp + 2, :].rearrange("p a f -> p (a f)")
 
-        prep_w(0)
-        stage_t(0)
-        for w in range(1, 5):
-            prep_w(w)
-        stage_t(1)
-        for s in range(NSB):
-            stage_m(s)
-            if s + 2 < NSB:
-                stage_t(s + 2)
-            stage_n(s)
+        def pbias(s, jp):
+            if ("pb", s) not in t:
+                t["pb", s] = outp.tile([P, JT, N_HID], F32, tag="pb", name="pb")
+            nc.vector.tensor_tensor(
+                out=half(t["pb", s], jp), in0=t["accp", s, jp][:], in1=bp_bc[:].rearrange("p a f -> p (a f)"), op=ALU.add
+            )
+
+        def dd(s, hf):
+            if ("d", s) not in t:
+                t["d", s] = ep.tile([P, 2, SB], F32, tag="d", name="d")
+            nc.vector.tensor_tensor(out=t["d", s][:, hf, :], in0=t["h", s][:, hf, :], in1=t["g", s][:, hf, :], op=ALU.subtract)
+
+        def ee(s, hf):
+            nc.vector.scalar_tensor_tensor(
+                out=t["d", s][:, hf, :], in0=t["f", s][:, hf, :], scalar=1.0, in1=t["d", s][:, hf, :], op0=ALU.add, op1=ALU.mult
+            )
+
+        def nn(s, hf):
+            if ("nh", s) not in t:
+                t["nh", s] = ep.tile([P, 2, SB], F32, tag="nh", name="nh")
+            nc.vector.scalar_tensor_tensor(
+                out=t["nh", s][:, hf, :], in0=t["d", s][:, hf, :], scalar=0.5, in1=t["g", s][:, hf, :], op0=ALU.mult, op1=ALU.add
+            )
+
+        def nt(s, jp):
+            bank = tr.tile([P, 512], F32, tag="tr", name="nt")
+            t["nt", s, jp] = bank
+            for jj in range(2):
+                j = 2 * jp + jj
+                for hf in range(2):
+                    o = N_HID * jj + P * hf
+                    nc.tensor.transpose(bank[:, o : o + P], t["nh", s][:, hf, P * j : P * (j + 1)], ident[:])
+
+        def ncp(s, jp, eng):
+            if ("nht", s) not in t:
+                t["nht", s] = outp.tile([P, JT, N_HID], F32, tag="nht", name="nht")
+            copy_on(eng, half(t["nht", s], jp), t["nt", s, jp][:])
+
+        def yh(s, jp):
+            if ("y", s) not in t:
+                t["y", s] = outp.tile([P, JT, N_HID], F32, tag="y", name="y")
+            nc.vector.tensor_tensor(out=half(t["y", s], jp), in0=half(t["nht", s], jp), in1=half(t["pb", s], jp), op=ALU.add)
+
+        def yy(s):
+            t["y", s] = outp.tile([P, JT, N_HID], F32, tag="y", name="y")
+            nc.vector.tensor_tensor(out=t["y", s][:], in0=t["nht", s][:], in1=t["pb", s][:], op=ALU.add)
+
+        def store(dst, key, s, jp):
+            view = dst[SB * s : SB * (s + 1), :].rearrange("(p j) f -> p j f", j=JT)
+            if jp is None:
+                nc.sync.dma_start(out=view, in_=t[key, s][:])
+            else:
+                nc.sync.dma_start(out=view[:, 2 * jp : 2 * jp + 2, :], in_=t[key, s][:, 2 * jp : 2 * jp + 2, :])
+
+        xt(0, 0)
+        xcp(0, 0, "S")
+        xt(0, 1)
+        xcp(0, 1, "S")
+        xt(0, 2)
+        xcp(0, 2, "S")
+        xt(0, 3)
+        xcp(0, 3, "S")
+        mm(0, 0)
+        mm(0, 1)
+        wt(0, 0)
+        wcp(0, 0, "S")
+        wt(0, 1)
+        wcp(0, 1, "S")
+        mm(1, 0)
+        mm(1, 1)
+        wt(1, 0)
+        wcp(1, 0, "S")
+        wt(1, 1)
+        wcp(1, 1, "S")
+        mm(2, 0)
+        mm(2, 1)
+        wq(0)
+        xqz(0)
+        wt(2, 0)
+        wcp(2, 0, "S")
+        wt(2, 1)
+        wcp(2, 1, "S")
+        mm(3, 0)
+        mm(3, 1)
+        wq(1)
+        mxl(0, "g", 0)
+        actl(0, "g", 0)
+        mxl(0, "g", 1)
+        actl(0, "g", 1)
+        wt(3, 0)
+        wcp(3, 0, "S")
+        wt(3, 1)
+        wcp(3, 1, "S")
+        mm(4, 0)
+        mm(4, 1)
+        wq(2)
+        mxl(0, "h", 0)
+        actl(0, "h", 0)
+        mxl(0, "h", 1)
+        actl(0, "h", 1)
+        wt(4, 0)
+        wcp(4, 0, "S")
+        wt(4, 1)
+        wcp(4, 1, "S")
+        wq(3)
+        xt(1, 0)
+        xcp(1, 0, "S")
+        xt(1, 1)
+        xcp(1, 1, "S")
+        xt(1, 2)
+        xcp(1, 2, "S")
+        xt(1, 3)
+        xcp(1, 3, "S")
+        wq(4)
+        mxl(0, "f", 0)
+        actl(0, "f", 0)
+        mxl(0, "f", 1)
+        actl(0, "f", 1)
+        xqz(1)
+        mxp(0, 0)
+        mxp(0, 1)
+        dd(0, 0)
+        dd(0, 1)
+        ee(0, 0)
+        pbias(0, 0)
+        ee(0, 1)
+        pbias(0, 1)
+        nn(0, 0)
+        nn(0, 1)
+        xt(2, 0)
+        xcp(2, 0, "S")
+        xt(2, 1)
+        xcp(2, 1, "S")
+        xt(2, 2)
+        xcp(2, 2, "S")
+        xt(2, 3)
+        xcp(2, 3, "S")
+        mxl(1, "g", 0)
+        actl(1, "g", 0)
+        mxl(1, "h", 0)
+        actl(1, "h", 0)
+        xqz(2)
+        mxl(1, "f", 0)
+        actl(1, "f", 0)
+        mxl(1, "g", 1)
+        actl(1, "g", 1)
+        dd(1, 0)
+        mxl(1, "h", 1)
+        actl(1, "h", 1)
+        ee(1, 0)
+        mxl(1, "f", 1)
+        actl(1, "f", 1)
+        dd(1, 1)
+        nn(1, 0)
+        mxp(1, 0)
+        mxp(1, 1)
+        ee(1, 1)
+        pbias(1, 0)
+        nn(1, 1)
+        pbias(1, 1)
+        nt(0, 0)
+        ncp(0, 0, "S")
+        nt(0, 1)
+        ncp(0, 1, "S")
+        xt(3, 0)
+        xcp(3, 0, "S")
+        xt(3, 1)
+        xcp(3, 1, "S")
+        xt(3, 2)
+        xcp(3, 2, "S")
+        xt(3, 3)
+        xcp(3, 3, "S")
+        mxl(2, "g", 0)
+        actl(2, "g", 0)
+        mxl(2, "h", 0)
+        actl(2, "h", 0)
+        xqz(3)
+        mxl(2, "f", 0)
+        actl(2, "f", 0)
+        yy(0)
+        store(out_1, "nht", 0, None)
+        store(out_0, "y", 0, None)
+        mxl(2, "g", 1)
+        actl(2, "g", 1)
+        dd(2, 0)
+        mxl(2, "h", 1)
+        actl(2, "h", 1)
+        ee(2, 0)
+        mxl(2, "f", 1)
+        actl(2, "f", 1)
+        dd(2, 1)
+        nn(2, 0)
+        mxp(2, 0)
+        mxp(2, 1)
+        ee(2, 1)
+        pbias(2, 0)
+        nn(2, 1)
+        pbias(2, 1)
+        nt(1, 0)
+        ncp(1, 0, "S")
+        nt(1, 1)
+        ncp(1, 1, "S")
+        xt(4, 0)
+        xcp(4, 0, "S")
+        xt(4, 1)
+        xcp(4, 1, "S")
+        xt(4, 2)
+        xcp(4, 2, "S")
+        xt(4, 3)
+        xcp(4, 3, "S")
+        mxl(3, "g", 0)
+        actl(3, "g", 0)
+        mxl(3, "h", 0)
+        actl(3, "h", 0)
+        xqz(4)
+        mxl(3, "f", 0)
+        actl(3, "f", 0)
+        yy(1)
+        store(out_1, "nht", 1, None)
+        store(out_0, "y", 1, None)
+        mxl(3, "g", 1)
+        actl(3, "g", 1)
+        dd(3, 0)
+        mxl(3, "h", 1)
+        actl(3, "h", 1)
+        ee(3, 0)
+        mxl(3, "f", 1)
+        actl(3, "f", 1)
+        dd(3, 1)
+        nn(3, 0)
+        mxp(3, 0)
+        mxp(3, 1)
+        ee(3, 1)
+        pbias(3, 0)
+        nn(3, 1)
+        pbias(3, 1)
+        nt(2, 0)
+        ncp(2, 0, "S")
+        nt(2, 1)
+        ncp(2, 1, "S")
+        xt(5, 0)
+        xcp(5, 0, "S")
+        xt(5, 1)
+        xcp(5, 1, "S")
+        xt(5, 2)
+        xcp(5, 2, "S")
+        xt(5, 3)
+        xcp(5, 3, "S")
+        mxl(4, "g", 0)
+        actl(4, "g", 0)
+        mxl(4, "h", 0)
+        actl(4, "h", 0)
+        xqz(5)
+        mxl(4, "f", 0)
+        actl(4, "f", 0)
+        yy(2)
+        store(out_1, "nht", 2, None)
+        store(out_0, "y", 2, None)
+        mxl(4, "g", 1)
+        actl(4, "g", 1)
+        dd(4, 0)
+        mxl(4, "h", 1)
+        actl(4, "h", 1)
+        ee(4, 0)
+        mxl(4, "f", 1)
+        actl(4, "f", 1)
+        dd(4, 1)
+        nn(4, 0)
+        mxp(4, 0)
+        mxp(4, 1)
+        ee(4, 1)
+        pbias(4, 0)
+        nn(4, 1)
+        pbias(4, 1)
+        nt(3, 0)
+        ncp(3, 0, "S")
+        nt(3, 1)
+        ncp(3, 1, "S")
+        xt(6, 0)
+        xcp(6, 0, "S")
+        xt(6, 1)
+        xcp(6, 1, "S")
+        xt(6, 2)
+        xcp(6, 2, "S")
+        xt(6, 3)
+        xcp(6, 3, "S")
+        mxl(5, "g", 0)
+        actl(5, "g", 0)
+        mxl(5, "h", 0)
+        actl(5, "h", 0)
+        xqz(6)
+        mxl(5, "f", 0)
+        actl(5, "f", 0)
+        yy(3)
+        store(out_1, "nht", 3, None)
+        store(out_0, "y", 3, None)
+        mxl(5, "g", 1)
+        actl(5, "g", 1)
+        dd(5, 0)
+        mxl(5, "h", 1)
+        actl(5, "h", 1)
+        ee(5, 0)
+        mxl(5, "f", 1)
+        actl(5, "f", 1)
+        dd(5, 1)
+        nn(5, 0)
+        mxp(5, 0)
+        mxp(5, 1)
+        ee(5, 1)
+        pbias(5, 0)
+        nn(5, 1)
+        pbias(5, 1)
+        nt(4, 0)
+        ncp(4, 0, "S")
+        nt(4, 1)
+        ncp(4, 1, "S")
+        xt(7, 0)
+        xcp(7, 0, "S")
+        xt(7, 1)
+        xcp(7, 1, "S")
+        xt(7, 2)
+        xcp(7, 2, "S")
+        xt(7, 3)
+        xcp(7, 3, "S")
+        mxl(6, "g", 0)
+        actl(6, "g", 0)
+        mxl(6, "h", 0)
+        actl(6, "h", 0)
+        xqz(7)
+        mxl(6, "f", 0)
+        actl(6, "f", 0)
+        yy(4)
+        store(out_1, "nht", 4, None)
+        store(out_0, "y", 4, None)
+        mxl(6, "g", 1)
+        actl(6, "g", 1)
+        dd(6, 0)
+        mxl(6, "h", 1)
+        actl(6, "h", 1)
+        ee(6, 0)
+        mxl(6, "f", 1)
+        actl(6, "f", 1)
+        dd(6, 1)
+        nn(6, 0)
+        mxp(6, 0)
+        mxp(6, 1)
+        ee(6, 1)
+        pbias(6, 0)
+        nn(6, 1)
+        pbias(6, 1)
+        nt(5, 0)
+        ncp(5, 0, "S")
+        nt(5, 1)
+        ncp(5, 1, "S")
+        mxl(7, "g", 0)
+        actl(7, "g", 0)
+        mxl(7, "h", 0)
+        actl(7, "h", 0)
+        mxl(7, "f", 0)
+        actl(7, "f", 0)
+        yy(5)
+        store(out_1, "nht", 5, None)
+        store(out_0, "y", 5, None)
+        mxl(7, "g", 1)
+        actl(7, "g", 1)
+        dd(7, 0)
+        mxl(7, "h", 1)
+        actl(7, "h", 1)
+        ee(7, 0)
+        nt(6, 0)
+        ncp(6, 0, "S")
+        nt(6, 1)
+        ncp(6, 1, "S")
+        mxp(7, 0)
+        mxp(7, 1)
+        mxl(7, "f", 1)
+        actl(7, "f", 1)
+        dd(7, 1)
+        nn(7, 0)
+        pbias(7, 0)
+        pbias(7, 1)
+        yy(6)
+        store(out_1, "nht", 6, None)
+        store(out_0, "y", 6, None)
+        ee(7, 1)
+        nn(7, 1)
+        nt(7, 0)
+        ncp(7, 0, "S")
+        nt(7, 1)
+        ncp(7, 1, "V")
+        store(out_1, "nht", 7, 0)
+        yh(7, 0)
+        store(out_0, "y", 7, 0)
+        store(out_1, "nht", 7, 1)
+        yh(7, 1)
+        store(out_0, "y", 7, 1)

@@ -39,16 +39,19 @@ def tile_ncpliquidcell_t_kernel(
         mx = ctx.enter_context(tc.psum_pool(name="mx", bufs=4))
         ctx.enter_context(tc.manual_schedule())
 
+        zt_bf = const.tile([P, P], BF16)
+        nc.vector.memset(zt_bf[:], 0.0)
+        zb_bf = const.tile([P, N_HID], BF16)
+        nc.vector.memset(zb_bf[:], 0.0)
+        for i, b in enumerate([bg, bh, bfg, bfh]):
+            nc.scalar.dma_start(out=zt_bf[2 * i : 2 * i + 2, :], in_=b.rearrange("(r c) -> r c", r=2))
+        nc.scalar.dma_start(out=zb_bf[0:1, :], in_=bp.rearrange("(o c) -> o c", o=1))
         warm = const.tile([P, 1], F32)
         nc.vector.memset(warm[:], 0.0)
         warm2 = const.tile([P, 1], F32)
         nc.scalar.activation(out=warm2[:], in_=warm[:], func=ACT.Tanh)
         ident = const.tile([P, P], F32)
         make_identity(nc, ident[:])
-        zt_bf = const.tile([P, P], BF16)
-        nc.vector.memset(zt_bf[:], 0.0)
-        zb_bf = const.tile([P, N_HID], BF16)
-        nc.vector.memset(zb_bf[:], 0.0)
         ones_bf = const.tile([P, P], BF16)
         nc.vector.memset(ones_bf[:], 1.0)
 
@@ -82,29 +85,32 @@ def tile_ncpliquidcell_t_kernel(
         load_x(5)
         load_x(6)
         load_x(7)
-        for i, b in enumerate([bg, bh, bfg, bfh]):
-            nc.scalar.dma_start(out=zt_bf[2 * i : 2 * i + 2, :], in_=b.rearrange("(r c) -> r c", r=2))
-        nc.scalar.dma_start(out=zb_bf[0:1, :], in_=bp.rearrange("(o c) -> o c", o=1))
 
         zt = const.tile([P, P], F32)
-        nc.vector.tensor_copy(out=zt[:], in_=zt_bf[:])
-        bt = tr.tile([P, 512], F32, tag="tr")
-        nc.tensor.transpose(bt[:, 0:P], zt[:], ident[:])
         bias_sb = const.tile([P, 8], F32)
-        nc.vector.tensor_copy(out=bias_sb[:], in_=bt[:, 0:8])
         bf_sum = const.tile([P, 2], F32)
-        nc.vector.tensor_tensor(out=bf_sum[:], in0=bias_sb[:, 4:6], in1=bias_sb[:, 6:8], op=ALU.add)
         bf_half = const.tile([P, 2], F32)
-        nc.vector.tensor_scalar_mul(out=bf_half[:], in0=bf_sum[:], scalar1=0.5)
-        bb = tr.tile([P, 512], F32, tag="tr")
-        nc.tensor.matmul(out=bb[:, 0:N_HID], lhsT=ones_bf[:], rhs=zb_bf[:], start=True, stop=True)
         bp_bc = const.tile([P, 2, N_HID], F32)
-        for r in range(2):
-            nc.vector.tensor_copy(out=bp_bc[:, r, :], in_=bb[:, 0:N_HID])
+        t = {}
+
+        def bc():
+            nc.vector.tensor_copy(out=zt[:], in_=zt_bf[:])
+
+        def bt():
+            t["bt"] = tr.tile([P, 512], F32, tag="tr", name="bt")
+            nc.tensor.transpose(t["bt"][:, 0:P], zt[:], ident[:])
+            t["bb"] = tr.tile([P, 512], F32, tag="tr", name="bb")
+            nc.tensor.matmul(out=t["bb"][:, 0:N_HID], lhsT=ones_bf[:], rhs=zb_bf[:], start=True, stop=True)
+
+        def bv():
+            nc.vector.tensor_copy(out=bias_sb[:], in_=t["bt"][:, 0:8])
+            nc.vector.tensor_tensor(out=bf_sum[:], in0=bias_sb[:, 4:6], in1=bias_sb[:, 6:8], op=ALU.add)
+            nc.vector.tensor_scalar_mul(out=bf_half[:], in0=bf_sum[:], scalar1=0.5)
+            for r in range(2):
+                nc.vector.tensor_copy(out=bp_bc[:, r, :], in_=t["bb"][:, 0:N_HID])
 
         wc = [const.tile([P, 2, N_HID], U32, name="wc%d" % w, align_bytes=64) for w in range(5)]
         ws = [const.tile([P, 2, N_HID], U8, name="ws%d" % w, align_bytes=64) for w in range(5)]
-        t = {}
 
         def copy_on(eng, out, in_):
             if eng == "S":
@@ -270,89 +276,92 @@ def tile_ncpliquidcell_t_kernel(
             else:
                 nc.sync.dma_start(out=view[:, 2 * jp : 2 * jp + 2, :], in_=t[key, s][:, 2 * jp : 2 * jp + 2, :])
 
-        xt(0, 0)
-        xcp(0, 0, "S")
-        xt(0, 1)
-        xcp(0, 1, "S")
-        xt(0, 2)
-        xcp(0, 2, "S")
+        bc()
         xt(0, 3)
-        xcp(0, 3, "S")
+        bt()
+        xcp(0, 3, "V")
+        bv()
+        xt(0, 0)
         mm(0, 0)
         mm(0, 1)
+        xt(0, 2)
         wt(0, 0)
-        wcp(0, 0, "S")
-        wt(0, 1)
-        wcp(0, 1, "S")
         mm(1, 0)
+        xcp(0, 2, "S")
         mm(1, 1)
-        wt(1, 0)
-        wcp(1, 0, "S")
-        wt(1, 1)
-        wcp(1, 1, "S")
         mm(2, 0)
+        wt(0, 1)
+        xcp(0, 0, "S")
+        wt(1, 1)
+        wcp(0, 1, "S")
+        wcp(0, 0, "S")
+        xt(0, 1)
         mm(2, 1)
+        xcp(0, 1, "S")
+        wcp(1, 1, "S")
         wq(0)
         xqz(0)
         wt(2, 0)
-        wcp(2, 0, "S")
-        wt(2, 1)
-        wcp(2, 1, "S")
-        mm(3, 0)
         mm(3, 1)
-        wq(1)
+        mm(3, 0)
+        wt(1, 0)
+        wt(2, 1)
         mxl(0, "g", 0)
-        actl(0, "g", 0)
         mxl(0, "g", 1)
-        actl(0, "g", 1)
-        wt(3, 0)
-        wcp(3, 0, "S")
+        wcp(1, 0, "S")
+        wq(1)
+        wcp(2, 0, "S")
         wt(3, 1)
-        wcp(3, 1, "S")
         mm(4, 0)
         mm(4, 1)
-        wq(2)
+        wt(3, 0)
         mxl(0, "h", 0)
-        actl(0, "h", 0)
         mxl(0, "h", 1)
-        actl(0, "h", 1)
-        wt(4, 0)
-        wcp(4, 0, "S")
         wt(4, 1)
-        wcp(4, 1, "S")
-        wq(3)
-        xt(1, 0)
-        xcp(1, 0, "S")
-        xt(1, 1)
-        xcp(1, 1, "S")
+        wcp(3, 1, "V")
+        wcp(2, 1, "S")
+        actl(0, "g", 0)
+        wt(4, 0)
         xt(1, 2)
-        xcp(1, 2, "S")
+        wq(2)
+        wcp(3, 0, "S")
+        wcp(4, 0, "V")
+        wq(3)
+        wcp(4, 1, "S")
+        xt(1, 0)
         xt(1, 3)
-        xcp(1, 3, "S")
+        xt(1, 1)
         wq(4)
-        mxl(0, "f", 0)
-        actl(0, "f", 0)
+        xcp(1, 3, "V")
+        xcp(1, 2, "S")
+        xcp(1, 0, "S")
+        actl(0, "g", 1)
+        xt(2, 0)
         mxl(0, "f", 1)
+        xcp(1, 1, "V")
+        actl(0, "h", 0)
+        mxp(0, 1)
+        mxl(0, "f", 0)
+        actl(0, "h", 1)
         actl(0, "f", 1)
+        actl(0, "f", 0)
+        dd(0, 1)
         xqz(1)
         mxp(0, 0)
-        mxp(0, 1)
+        xcp(2, 0, "S")
         dd(0, 0)
-        dd(0, 1)
+        pbias(0, 1)
+        xt(2, 3)
+        xt(2, 2)
         ee(0, 0)
         pbias(0, 0)
         ee(0, 1)
-        pbias(0, 1)
-        nn(0, 0)
-        nn(0, 1)
-        xt(2, 0)
-        xcp(2, 0, "S")
         xt(2, 1)
-        xcp(2, 1, "S")
-        xt(2, 2)
         xcp(2, 2, "S")
-        xt(2, 3)
         xcp(2, 3, "S")
+        xcp(2, 1, "S")
+        nn(0, 1)
+        nn(0, 0)
         mxl(1, "g", 0)
         actl(1, "g", 0)
         mxl(1, "h", 0)
@@ -571,44 +580,44 @@ def tile_ncpliquidcell_t_kernel(
         nt(5, 1)
         ncp(5, 1, "S")
         mxl(7, "g", 0)
-        actl(7, "g", 0)
         mxl(7, "h", 0)
-        actl(7, "h", 0)
         mxl(7, "f", 0)
+        actl(7, "g", 0)
+        mxl(7, "g", 1)
+        actl(7, "h", 0)
         actl(7, "f", 0)
+        mxl(7, "h", 1)
+        nt(6, 0)
+        dd(7, 0)
         yy(5)
+        ee(7, 0)
+        nt(6, 1)
+        actl(7, "g", 1)
+        actl(7, "h", 1)
         store(out_1, "nht", 5, None)
         store(out_0, "y", 5, None)
-        mxl(7, "g", 1)
-        actl(7, "g", 1)
-        dd(7, 0)
-        mxl(7, "h", 1)
-        actl(7, "h", 1)
-        ee(7, 0)
-        nt(6, 0)
-        ncp(6, 0, "S")
-        nt(6, 1)
-        ncp(6, 1, "S")
-        mxp(7, 0)
-        mxp(7, 1)
         mxl(7, "f", 1)
-        actl(7, "f", 1)
         dd(7, 1)
+        ncp(6, 0, "S")
+        ncp(6, 1, "S")
+        actl(7, "f", 1)
+        mxp(7, 1)
         nn(7, 0)
-        pbias(7, 0)
-        pbias(7, 1)
         yy(6)
         store(out_1, "nht", 6, None)
         store(out_0, "y", 6, None)
+        mxp(7, 0)
         ee(7, 1)
         nn(7, 1)
+        pbias(7, 0)
         nt(7, 0)
+        pbias(7, 1)
         ncp(7, 0, "S")
         nt(7, 1)
-        ncp(7, 1, "V")
         store(out_1, "nht", 7, 0)
+        ncp(7, 1, "S")
         yh(7, 0)
-        store(out_0, "y", 7, 0)
         store(out_1, "nht", 7, 1)
+        store(out_0, "y", 7, 0)
         yh(7, 1)
         store(out_0, "y", 7, 1)

@@ -276,348 +276,348 @@ def tile_ncpliquidcell_t_kernel(
             else:
                 nc.sync.dma_start(out=view[:, 2 * jp : 2 * jp + 2, :], in_=t[key, s][:, 2 * jp : 2 * jp + 2, :])
 
-        bc()
-        xt(0, 3)
-        bt()
-        xcp(0, 3, "V")
-        bv()
-        xt(0, 0)
-        mm(0, 0)
-        mm(0, 1)
         xt(0, 2)
-        wt(0, 0)
-        mm(1, 0)
+        bc()
         xcp(0, 2, "S")
-        mm(1, 1)
-        mm(2, 0)
-        wt(0, 1)
+        bt()
+        xt(0, 0)
+        bv()
+        xt(0, 3)
+        mm(0, 0)
+        wt(0, 0)
+        mm(0, 1)
         xcp(0, 0, "S")
+        mm(1, 1)
+        mm(1, 0)
+        xt(0, 1)
+        wt(0, 1)
+        wcp(0, 0, "S")
+        mm(2, 0)
+        xcp(0, 3, "S")
         wt(1, 1)
         wcp(0, 1, "S")
-        wcp(0, 0, "S")
-        xt(0, 1)
         mm(2, 1)
         xcp(0, 1, "S")
         wcp(1, 1, "S")
         wq(0)
-        xqz(0)
         wt(2, 0)
-        mm(3, 1)
-        mm(3, 0)
+        xqz(0)
         wt(1, 0)
+        wcp(1, 0, "S")
         wt(2, 1)
         mxl(0, "g", 0)
-        mxl(0, "g", 1)
-        wcp(1, 0, "S")
-        wq(1)
-        wcp(2, 0, "S")
-        wt(3, 1)
-        mm(4, 0)
-        mm(4, 1)
-        wt(3, 0)
-        mxl(0, "h", 0)
-        mxl(0, "h", 1)
-        wt(4, 1)
-        wcp(3, 1, "V")
         wcp(2, 1, "S")
+        wcp(2, 0, "S")
+        wq(1)
+        mm(4, 0)
+        mxl(0, "h", 1)
+        mm(3, 1)
+        mm(3, 0)
+        mm(4, 1)
+        mxl(0, "g", 1)
+        wt(3, 1)
         actl(0, "g", 0)
-        wt(4, 0)
-        xt(1, 2)
-        wq(2)
-        wcp(3, 0, "S")
-        wcp(4, 0, "V")
-        wq(3)
-        wcp(4, 1, "S")
-        xt(1, 0)
-        xt(1, 3)
-        xt(1, 1)
-        wq(4)
-        xcp(1, 3, "V")
-        xcp(1, 2, "S")
-        xcp(1, 0, "S")
+        wt(3, 0)
         actl(0, "g", 1)
-        xt(2, 0)
-        mxl(0, "f", 1)
-        xcp(1, 1, "V")
-        actl(0, "h", 0)
-        mxp(0, 1)
-        mxl(0, "f", 0)
+        wcp(3, 1, "S")
+        wq(2)
+        wt(4, 1)
+        wcp(3, 0, "V")
+        wt(4, 0)
+        mxl(0, "h", 0)
+        wcp(4, 1, "S")
+        wcp(4, 0, "V")
+        xt(1, 1)
+        wq(3)
         actl(0, "h", 1)
-        actl(0, "f", 1)
-        actl(0, "f", 0)
+        wq(4)
+        xt(1, 3)
+        xt(1, 0)
+        xt(1, 2)
         dd(0, 1)
-        xqz(1)
+        xcp(1, 1, "V")
+        xcp(1, 3, "S")
+        mxl(0, "f", 0)
+        xcp(1, 0, "S")
+        actl(0, "h", 0)
+        mxl(0, "f", 1)
+        mxp(0, 1)
+        xcp(1, 2, "S")
         mxp(0, 0)
-        xcp(2, 0, "S")
         dd(0, 0)
-        pbias(0, 1)
+        xqz(1)
         xt(2, 3)
+        actl(0, "f", 1)
         xt(2, 2)
+        pbias(0, 1)
+        actl(0, "f", 0)
         ee(0, 0)
         pbias(0, 0)
         ee(0, 1)
+        nn(0, 1)
         xt(2, 1)
         xcp(2, 2, "S")
-        xcp(2, 3, "S")
-        xcp(2, 1, "S")
-        nn(0, 1)
+        xt(2, 0)
         nn(0, 0)
+        xcp(2, 1, "S")
+        xcp(2, 0, "S")
+        xcp(2, 3, "S")
         mxl(1, "g", 0)
-        actl(1, "g", 0)
         mxl(1, "h", 0)
-        actl(1, "h", 0)
-        xqz(2)
         mxl(1, "f", 0)
+        actl(1, "g", 0)
+        nt(0, 0)
+        nt(0, 1)
+        xt(3, 0)
+        xqz(2)
+        actl(1, "h", 0)
+        dd(1, 0)
         actl(1, "f", 0)
         mxl(1, "g", 1)
-        actl(1, "g", 1)
-        dd(1, 0)
         mxl(1, "h", 1)
-        actl(1, "h", 1)
         ee(1, 0)
-        mxl(1, "f", 1)
-        actl(1, "f", 1)
-        dd(1, 1)
-        nn(1, 0)
-        mxp(1, 0)
-        mxp(1, 1)
-        ee(1, 1)
-        pbias(1, 0)
-        nn(1, 1)
-        pbias(1, 1)
-        nt(0, 0)
         ncp(0, 0, "S")
-        nt(0, 1)
+        mxl(1, "f", 1)
+        mxp(1, 0)
         ncp(0, 1, "S")
-        xt(3, 0)
+        nn(1, 0)
         xcp(3, 0, "S")
-        xt(3, 1)
-        xcp(3, 1, "S")
-        xt(3, 2)
-        xcp(3, 2, "S")
-        xt(3, 3)
-        xcp(3, 3, "S")
-        mxl(2, "g", 0)
-        actl(2, "g", 0)
-        mxl(2, "h", 0)
-        actl(2, "h", 0)
-        xqz(3)
-        mxl(2, "f", 0)
-        actl(2, "f", 0)
+        actl(1, "g", 1)
         yy(0)
+        actl(1, "h", 1)
         store(out_1, "nht", 0, None)
         store(out_0, "y", 0, None)
-        mxl(2, "g", 1)
-        actl(2, "g", 1)
-        dd(2, 0)
-        mxl(2, "h", 1)
-        actl(2, "h", 1)
-        ee(2, 0)
-        mxl(2, "f", 1)
-        actl(2, "f", 1)
-        dd(2, 1)
-        nn(2, 0)
-        mxp(2, 0)
-        mxp(2, 1)
-        ee(2, 1)
-        pbias(2, 0)
-        nn(2, 1)
-        pbias(2, 1)
+        mxp(1, 1)
+        dd(1, 1)
+        xt(3, 1)
+        actl(1, "f", 1)
+        xcp(3, 1, "S")
+        xt(3, 2)
+        pbias(1, 0)
+        ee(1, 1)
+        xt(3, 3)
+        pbias(1, 1)
+        xcp(3, 2, "S")
+        nn(1, 1)
+        xcp(3, 3, "S")
+        mxl(2, "g", 0)
+        mxl(2, "h", 0)
+        mxl(2, "f", 0)
+        actl(2, "g", 0)
         nt(1, 0)
-        ncp(1, 0, "S")
         nt(1, 1)
-        ncp(1, 1, "S")
         xt(4, 0)
+        xqz(3)
+        actl(2, "h", 0)
+        dd(2, 0)
+        actl(2, "f", 0)
+        mxl(2, "g", 1)
+        mxl(2, "h", 1)
+        ee(2, 0)
+        ncp(1, 0, "S")
+        mxl(2, "f", 1)
+        mxp(2, 0)
+        ncp(1, 1, "S")
+        nn(2, 0)
         xcp(4, 0, "S")
-        xt(4, 1)
-        xcp(4, 1, "S")
-        xt(4, 2)
-        xcp(4, 2, "S")
-        xt(4, 3)
-        xcp(4, 3, "S")
-        mxl(3, "g", 0)
-        actl(3, "g", 0)
-        mxl(3, "h", 0)
-        actl(3, "h", 0)
-        xqz(4)
-        mxl(3, "f", 0)
-        actl(3, "f", 0)
+        actl(2, "g", 1)
         yy(1)
+        actl(2, "h", 1)
         store(out_1, "nht", 1, None)
         store(out_0, "y", 1, None)
-        mxl(3, "g", 1)
-        actl(3, "g", 1)
-        dd(3, 0)
-        mxl(3, "h", 1)
-        actl(3, "h", 1)
-        ee(3, 0)
-        mxl(3, "f", 1)
-        actl(3, "f", 1)
-        dd(3, 1)
-        nn(3, 0)
-        mxp(3, 0)
-        mxp(3, 1)
-        ee(3, 1)
-        pbias(3, 0)
-        nn(3, 1)
-        pbias(3, 1)
+        mxp(2, 1)
+        dd(2, 1)
+        xt(4, 1)
+        actl(2, "f", 1)
+        xcp(4, 1, "S")
+        xt(4, 2)
+        pbias(2, 0)
+        ee(2, 1)
+        xt(4, 3)
+        pbias(2, 1)
+        xcp(4, 2, "S")
+        nn(2, 1)
+        xcp(4, 3, "S")
+        mxl(3, "g", 0)
+        mxl(3, "h", 0)
+        mxl(3, "f", 0)
+        actl(3, "g", 0)
         nt(2, 0)
-        ncp(2, 0, "S")
         nt(2, 1)
-        ncp(2, 1, "S")
         xt(5, 0)
+        xqz(4)
+        actl(3, "h", 0)
+        dd(3, 0)
+        actl(3, "f", 0)
+        mxl(3, "g", 1)
+        mxl(3, "h", 1)
+        ee(3, 0)
+        ncp(2, 0, "S")
+        mxl(3, "f", 1)
+        mxp(3, 0)
+        ncp(2, 1, "S")
+        nn(3, 0)
         xcp(5, 0, "S")
-        xt(5, 1)
-        xcp(5, 1, "S")
-        xt(5, 2)
-        xcp(5, 2, "S")
-        xt(5, 3)
-        xcp(5, 3, "S")
-        mxl(4, "g", 0)
-        actl(4, "g", 0)
-        mxl(4, "h", 0)
-        actl(4, "h", 0)
-        xqz(5)
-        mxl(4, "f", 0)
-        actl(4, "f", 0)
+        actl(3, "g", 1)
         yy(2)
+        actl(3, "h", 1)
         store(out_1, "nht", 2, None)
         store(out_0, "y", 2, None)
-        mxl(4, "g", 1)
-        actl(4, "g", 1)
-        dd(4, 0)
-        mxl(4, "h", 1)
-        actl(4, "h", 1)
-        ee(4, 0)
-        mxl(4, "f", 1)
-        actl(4, "f", 1)
-        dd(4, 1)
-        nn(4, 0)
-        mxp(4, 0)
-        mxp(4, 1)
-        ee(4, 1)
-        pbias(4, 0)
-        nn(4, 1)
-        pbias(4, 1)
+        mxp(3, 1)
+        dd(3, 1)
+        xt(5, 1)
+        actl(3, "f", 1)
+        xcp(5, 1, "S")
+        xt(5, 2)
+        pbias(3, 0)
+        ee(3, 1)
+        xt(5, 3)
+        pbias(3, 1)
+        xcp(5, 2, "S")
+        nn(3, 1)
+        xcp(5, 3, "S")
+        mxl(4, "g", 0)
+        mxl(4, "h", 0)
+        mxl(4, "f", 0)
+        actl(4, "g", 0)
         nt(3, 0)
-        ncp(3, 0, "S")
         nt(3, 1)
-        ncp(3, 1, "S")
         xt(6, 0)
+        xqz(5)
+        actl(4, "h", 0)
+        dd(4, 0)
+        actl(4, "f", 0)
+        mxl(4, "g", 1)
+        mxl(4, "h", 1)
+        ee(4, 0)
+        ncp(3, 0, "S")
+        mxl(4, "f", 1)
+        mxp(4, 0)
+        ncp(3, 1, "S")
+        nn(4, 0)
         xcp(6, 0, "S")
-        xt(6, 1)
-        xcp(6, 1, "S")
-        xt(6, 2)
-        xcp(6, 2, "S")
-        xt(6, 3)
-        xcp(6, 3, "S")
-        mxl(5, "g", 0)
-        actl(5, "g", 0)
-        mxl(5, "h", 0)
-        actl(5, "h", 0)
-        xqz(6)
-        mxl(5, "f", 0)
-        actl(5, "f", 0)
+        actl(4, "g", 1)
         yy(3)
+        actl(4, "h", 1)
         store(out_1, "nht", 3, None)
         store(out_0, "y", 3, None)
-        mxl(5, "g", 1)
-        actl(5, "g", 1)
-        dd(5, 0)
-        mxl(5, "h", 1)
-        actl(5, "h", 1)
-        ee(5, 0)
-        mxl(5, "f", 1)
-        actl(5, "f", 1)
-        dd(5, 1)
-        nn(5, 0)
-        mxp(5, 0)
-        mxp(5, 1)
-        ee(5, 1)
-        pbias(5, 0)
-        nn(5, 1)
-        pbias(5, 1)
+        mxp(4, 1)
+        dd(4, 1)
+        xt(6, 1)
+        actl(4, "f", 1)
+        xcp(6, 1, "S")
+        xt(6, 2)
+        pbias(4, 0)
+        ee(4, 1)
+        xt(6, 3)
+        pbias(4, 1)
+        xcp(6, 2, "S")
+        nn(4, 1)
+        xcp(6, 3, "S")
+        mxl(5, "g", 0)
+        mxl(5, "h", 0)
+        mxl(5, "f", 0)
+        actl(5, "g", 0)
         nt(4, 0)
-        ncp(4, 0, "S")
         nt(4, 1)
-        ncp(4, 1, "S")
         xt(7, 0)
+        xqz(6)
+        actl(5, "h", 0)
+        dd(5, 0)
+        actl(5, "f", 0)
+        mxl(5, "g", 1)
+        mxl(5, "h", 1)
+        ee(5, 0)
+        ncp(4, 0, "S")
+        mxl(5, "f", 1)
+        mxp(5, 0)
+        ncp(4, 1, "S")
+        nn(5, 0)
         xcp(7, 0, "S")
-        xt(7, 1)
-        xcp(7, 1, "S")
-        xt(7, 2)
-        xcp(7, 2, "S")
-        xt(7, 3)
-        xcp(7, 3, "S")
-        mxl(6, "g", 0)
-        actl(6, "g", 0)
-        mxl(6, "h", 0)
-        actl(6, "h", 0)
-        xqz(7)
-        mxl(6, "f", 0)
-        actl(6, "f", 0)
+        actl(5, "g", 1)
         yy(4)
+        actl(5, "h", 1)
         store(out_1, "nht", 4, None)
         store(out_0, "y", 4, None)
-        mxl(6, "g", 1)
-        actl(6, "g", 1)
-        dd(6, 0)
-        mxl(6, "h", 1)
-        actl(6, "h", 1)
-        ee(6, 0)
-        mxl(6, "f", 1)
-        actl(6, "f", 1)
-        dd(6, 1)
-        nn(6, 0)
-        mxp(6, 0)
-        mxp(6, 1)
-        ee(6, 1)
-        pbias(6, 0)
-        nn(6, 1)
-        pbias(6, 1)
+        mxp(5, 1)
+        dd(5, 1)
+        xt(7, 1)
+        actl(5, "f", 1)
+        xcp(7, 1, "S")
+        xt(7, 2)
+        pbias(5, 0)
+        ee(5, 1)
+        xt(7, 3)
+        pbias(5, 1)
+        xcp(7, 2, "S")
+        nn(5, 1)
+        xcp(7, 3, "S")
+        mxl(6, "g", 0)
+        mxl(6, "h", 0)
+        mxl(6, "f", 0)
+        actl(6, "g", 0)
         nt(5, 0)
-        ncp(5, 0, "S")
         nt(5, 1)
+        xqz(7)
+        actl(6, "h", 0)
+        dd(6, 0)
+        actl(6, "f", 0)
+        mxl(6, "g", 1)
+        mxl(6, "h", 1)
+        ee(6, 0)
+        ncp(5, 0, "S")
+        mxl(6, "f", 1)
+        mxp(6, 0)
         ncp(5, 1, "S")
+        nn(6, 0)
+        actl(6, "g", 1)
+        yy(5)
+        actl(6, "h", 1)
+        store(out_1, "nht", 5, None)
+        store(out_0, "y", 5, None)
+        mxp(6, 1)
+        dd(6, 1)
+        actl(6, "f", 1)
+        pbias(6, 0)
+        ee(6, 1)
+        pbias(6, 1)
+        nn(6, 1)
         mxl(7, "g", 0)
         mxl(7, "h", 0)
         mxl(7, "f", 0)
         actl(7, "g", 0)
-        mxl(7, "g", 1)
         actl(7, "h", 0)
-        actl(7, "f", 0)
-        mxl(7, "h", 1)
         nt(6, 0)
-        dd(7, 0)
-        yy(5)
-        ee(7, 0)
         nt(6, 1)
-        actl(7, "g", 1)
-        actl(7, "h", 1)
-        store(out_1, "nht", 5, None)
-        store(out_0, "y", 5, None)
-        mxl(7, "f", 1)
-        dd(7, 1)
-        ncp(6, 0, "S")
+        actl(7, "f", 0)
+        mxl(7, "g", 1)
         ncp(6, 1, "S")
-        actl(7, "f", 1)
-        mxp(7, 1)
-        nn(7, 0)
+        dd(7, 0)
+        ncp(6, 0, "V")
+        actl(7, "g", 1)
+        mxl(7, "h", 1)
+        ee(7, 0)
+        actl(7, "h", 1)
         yy(6)
+        dd(7, 1)
+        mxl(7, "f", 1)
         store(out_1, "nht", 6, None)
         store(out_0, "y", 6, None)
+        actl(7, "f", 1)
+        mxp(7, 1)
         mxp(7, 0)
+        nn(7, 0)
         ee(7, 1)
         nn(7, 1)
-        pbias(7, 0)
         nt(7, 0)
-        pbias(7, 1)
         ncp(7, 0, "S")
-        nt(7, 1)
+        pbias(7, 1)
         store(out_1, "nht", 7, 0)
+        pbias(7, 0)
+        nt(7, 1)
         ncp(7, 1, "S")
         yh(7, 0)
         store(out_1, "nht", 7, 1)
-        store(out_0, "y", 7, 0)
         yh(7, 1)
+        store(out_0, "y", 7, 0)
         store(out_0, "y", 7, 1)

@@ -27,7 +27,7 @@ def tile_ncpliquidcell_t_kernel(
     weights = [Wg, Wh, Wfg, Wfh, Wp]
     with ExitStack() as ctx:
         const = ctx.enter_context(tc.tile_pool(name="const", bufs=1))
-        wraw = ctx.enter_context(tc.tile_pool(name="wraw", bufs=5))
+        wraw = ctx.enter_context(tc.tile_pool(name="wraw", bufs=10))
         wgr = ctx.enter_context(tc.tile_pool(name="wgr", bufs=2))
         xin = ctx.enter_context(tc.tile_pool(name="xin", bufs=NSB))
         xgr = ctx.enter_context(tc.tile_pool(name="xgr", bufs=2))
@@ -55,16 +55,16 @@ def tile_ncpliquidcell_t_kernel(
         ones_bf = const.tile([P, P], BF16)
         nc.vector.memset(ones_bf[:], 1.0)
 
-        mask_sb = const.tile([P, 2, K], BF16)
-        w_sb = [wraw.tile([P, 2, K], BF16, name="w%d" % w, tag="w") for w in range(5)]
+        mask_sb = [const.tile([P, K], BF16, name="mask%d" % hf) for hf in range(2)]
+        w_sb = [[wraw.tile([P, K], BF16, name="w%d_%d" % (w, hf), tag="w") for hf in range(2)] for w in range(5)]
         x_sb = [xin.tile([P, JT, IN_F], BF16, name="x%d" % s, tag="x") for s in range(NSB)]
         h_sb = [xin.tile([P, JT, N_HID], BF16, name="h%d" % s, tag="h") for s in range(NSB)]
 
-        def load_m():
-            nc.sync.dma_start(out=mask_sb[:], in_=mask.rearrange("(h p) k -> p h k", p=P))
+        def load_m(hf):
+            nc.sync.dma_start(out=mask_sb[hf][:], in_=mask[P * hf : P * (hf + 1), :])
 
-        def load_w(w):
-            nc.sync.dma_start(out=w_sb[w][:], in_=weights[w].rearrange("(h p) k -> p h k", p=P))
+        def load_w(w, hf):
+            nc.sync.dma_start(out=w_sb[w][hf][:], in_=weights[w][P * hf : P * (hf + 1), :])
 
         def load_x(s):
             rows = slice(SB * s, SB * (s + 1))
@@ -72,13 +72,19 @@ def tile_ncpliquidcell_t_kernel(
             nc.sync.dma_start(out=h_sb[s][:], in_=hidden[rows, :].rearrange("(p j) k -> p j k", j=JT))
 
         load_x(0)
-        load_m()
-        load_w(0)
-        load_w(1)
-        load_w(2)
-        load_w(3)
-        load_w(4)
+        load_m(0)
+        load_w(0, 0)
+        load_m(1)
+        load_w(0, 1)
+        load_w(1, 0)
+        load_w(1, 1)
         load_x(1)
+        load_w(2, 0)
+        load_w(2, 1)
+        load_w(3, 0)
+        load_w(3, 1)
+        load_w(4, 0)
+        load_w(4, 1)
         load_x(2)
         load_x(3)
         load_x(4)
@@ -119,12 +125,12 @@ def tile_ncpliquidcell_t_kernel(
                 nc.vector.tensor_copy(out=out, in_=in_)
 
         def mm(w, hf):
-            nc.vector.tensor_tensor(out=w_sb[w][:, hf, :], in0=w_sb[w][:, hf, :], in1=mask_sb[:, hf, :], op=ALU.mult)
+            nc.vector.tensor_tensor(out=w_sb[w][hf][:], in0=w_sb[w][hf][:], in1=mask_sb[hf][:], op=ALU.mult)
 
         def wt(w, hf):
             bank = tr.tile([P, 512], F32, tag="tr", name="wt")
             t["wt", w, hf] = bank
-            ww = w_sb[w][:, hf, :].bitcast(F32)
+            ww = w_sb[w][hf][:].bitcast(F32)
             for b in range(4):
                 nc.tensor.transpose(bank[:, P * b : P * (b + 1)], ww[:, P * b : P * (b + 1)], ident[:])
 
@@ -203,6 +209,31 @@ def tile_ncpliquidcell_t_kernel(
                 bias, scale = bf_half[:, hf : hf + 1], 0.5
             nc.scalar.activation(out=t[lay, s][:, hf, :], in_=t["acc", s, lay, hf][:], func=ACT.Tanh, bias=bias, scale=scale)
 
+        def actf2(s, k):
+            hf, c = k // 2, k % 2
+            cols = slice(N_HID * c, N_HID * (c + 1))
+            if ("f", s) not in t:
+                t["f", s] = act.tile([P, 2, SB], F32, tag="f", name="af")
+            nc.scalar.activation(
+                out=t["f", s][:, hf, cols], in_=t["acc", s, "f", hf][:, cols], func=ACT.Tanh, bias=bf_half[:, hf : hf + 1], scale=0.5
+            )
+
+        def ee2(s, k):
+            hf, c = k // 2, k % 2
+            cols = slice(N_HID * c, N_HID * (c + 1))
+            nc.vector.scalar_tensor_tensor(
+                out=t["d", s][:, hf, cols], in0=t["f", s][:, hf, cols], scalar=1.0, in1=t["d", s][:, hf, cols], op0=ALU.add, op1=ALU.mult
+            )
+
+        def nn2(s, k):
+            hf, c = k // 2, k % 2
+            cols = slice(N_HID * c, N_HID * (c + 1))
+            if ("nh", s) not in t:
+                t["nh", s] = ep.tile([P, 2, SB], F32, tag="nh", name="nh")
+            nc.vector.scalar_tensor_tensor(
+                out=t["nh", s][:, hf, cols], in0=t["d", s][:, hf, cols], scalar=0.5, in1=t["g", s][:, hf, cols], op0=ALU.mult, op1=ALU.add
+            )
+
         def mxp(s, jp):
             acc = mx.tile([P, 512], F32, tag="mx", name="accp")
             t["accp", s, jp] = acc
@@ -276,92 +307,92 @@ def tile_ncpliquidcell_t_kernel(
             else:
                 nc.sync.dma_start(out=view[:, 2 * jp : 2 * jp + 2, :], in_=t[key, s][:, 2 * jp : 2 * jp + 2, :])
 
-        xt(0, 2)
         bc()
-        xcp(0, 2, "S")
         bt()
-        xt(0, 0)
         bv()
-        xt(0, 3)
-        mm(0, 0)
-        wt(0, 0)
-        mm(0, 1)
-        xcp(0, 0, "S")
-        mm(1, 1)
-        mm(1, 0)
+        xt(0, 0)
         xt(0, 1)
-        wt(0, 1)
-        wcp(0, 0, "S")
-        mm(2, 0)
-        xcp(0, 3, "S")
-        wt(1, 1)
-        wcp(0, 1, "S")
-        mm(2, 1)
+        xt(0, 3)
         xcp(0, 1, "S")
-        wcp(1, 1, "S")
-        wq(0)
-        wt(2, 0)
-        xqz(0)
+        xcp(0, 0, "V")
+        mm(0, 0)
+        mm(0, 1)
+        xt(0, 2)
+        wt(0, 0)
+        wt(0, 1)
+        xcp(0, 3, "S")
+        mm(1, 0)
+        mm(1, 1)
+        wcp(0, 0, "S")
+        xcp(0, 2, "S")
+        wcp(0, 1, "S")
         wt(1, 0)
+        wt(1, 1)
+        wcp(1, 1, "S")
+        xqz(0)
+        wq(0)
+        mm(2, 0)
+        xt(1, 3)
         wcp(1, 0, "S")
-        wt(2, 1)
-        mxl(0, "g", 0)
-        wcp(2, 1, "S")
-        wcp(2, 0, "S")
         wq(1)
-        mm(4, 0)
-        mxl(0, "h", 1)
-        mm(3, 1)
-        mm(3, 0)
-        mm(4, 1)
+        mm(2, 1)
         mxl(0, "g", 1)
-        wt(3, 1)
-        actl(0, "g", 0)
-        wt(3, 0)
+        xcp(1, 3, "S")
         actl(0, "g", 1)
+        wt(2, 0)
+        mxl(0, "h", 1)
+        mxl(0, "g", 0)
+        actl(0, "h", 1)
+        mm(3, 1)
+        wt(3, 1)
+        mm(3, 0)
+        wcp(2, 0, "S")
+        mm(4, 0)
+        xt(1, 1)
+        mm(4, 1)
         wcp(3, 1, "S")
+        actl(0, "g", 0)
+        wt(2, 1)
+        wcp(2, 1, "S")
+        wt(3, 0)
+        xcp(1, 1, "V")
+        mxl(0, "h", 0)
+        xt(1, 2)
+        wcp(3, 0, "V")
+        xt(1, 0)
         wq(2)
         wt(4, 1)
-        wcp(3, 0, "V")
-        wt(4, 0)
-        mxl(0, "h", 0)
-        wcp(4, 1, "S")
-        wcp(4, 0, "V")
-        xt(1, 1)
         wq(3)
-        actl(0, "h", 1)
-        wq(4)
-        xt(1, 3)
-        xt(1, 0)
-        xt(1, 2)
-        dd(0, 1)
-        xcp(1, 1, "V")
-        xcp(1, 3, "S")
-        mxl(0, "f", 0)
-        xcp(1, 0, "S")
+        wt(4, 0)
         actl(0, "h", 0)
-        mxl(0, "f", 1)
-        mxp(0, 1)
-        xcp(1, 2, "S")
-        mxp(0, 0)
+        wcp(4, 1, "S")
+        wcp(4, 0, "S")
+        xcp(1, 0, "S")
+        mxl(0, "f", 0)
         dd(0, 0)
-        xqz(1)
-        xt(2, 3)
-        actl(0, "f", 1)
-        xt(2, 2)
-        pbias(0, 1)
+        mxl(0, "f", 1)
+        wq(4)
+        mxp(0, 0)
         actl(0, "f", 0)
+        dd(0, 1)
+        xcp(1, 2, "S")
         ee(0, 0)
-        pbias(0, 0)
-        ee(0, 1)
-        nn(0, 1)
-        xt(2, 1)
-        xcp(2, 2, "S")
-        xt(2, 0)
+        actl(0, "f", 1)
+        xqz(1)
         nn(0, 0)
-        xcp(2, 1, "S")
+        mxp(0, 1)
+        pbias(0, 0)
+        xt(2, 0)
+        ee(0, 1)
+        xt(2, 1)
         xcp(2, 0, "S")
+        xt(2, 3)
         xcp(2, 3, "S")
+        xcp(2, 1, "S")
+        pbias(0, 1)
+        xt(2, 2)
+        nn(0, 1)
+        xcp(2, 2, "S")
         mxl(1, "g", 0)
         mxl(1, "h", 0)
         mxl(1, "f", 0)
@@ -582,42 +613,45 @@ def tile_ncpliquidcell_t_kernel(
         ee(6, 1)
         pbias(6, 1)
         nn(6, 1)
-        mxl(7, "g", 0)
         mxl(7, "h", 0)
+        mxl(7, "g", 0)
         mxl(7, "f", 0)
-        actl(7, "g", 0)
         actl(7, "h", 0)
         nt(6, 0)
         nt(6, 1)
-        actl(7, "f", 0)
         mxl(7, "g", 1)
+        actl(7, "g", 0)
+        actl(7, "f", 0)
         ncp(6, 1, "S")
         dd(7, 0)
-        ncp(6, 0, "V")
-        actl(7, "g", 1)
         mxl(7, "h", 1)
-        ee(7, 0)
-        actl(7, "h", 1)
-        yy(6)
-        dd(7, 1)
+        actl(7, "g", 1)
+        ncp(6, 0, "V")
         mxl(7, "f", 1)
+        actl(7, "h", 1)
+        ee(7, 0)
+        yy(6)
+        actf2(7, 2)
+        dd(7, 1)
+        nn(7, 0)
+        mxp(7, 0)
+        actf2(7, 3)
+        ee2(7, 2)
+        ee2(7, 3)
+        mxp(7, 1)
+        nn2(7, 2)
+        nt(7, 0)
+        nn2(7, 3)
         store(out_1, "nht", 6, None)
         store(out_0, "y", 6, None)
-        actl(7, "f", 1)
-        mxp(7, 1)
-        mxp(7, 0)
-        nn(7, 0)
-        ee(7, 1)
-        nn(7, 1)
-        nt(7, 0)
-        ncp(7, 0, "S")
-        pbias(7, 1)
-        store(out_1, "nht", 7, 0)
         pbias(7, 0)
         nt(7, 1)
+        ncp(7, 0, "S")
         ncp(7, 1, "S")
+        pbias(7, 1)
         yh(7, 0)
+        store(out_1, "nht", 7, 0)
         store(out_1, "nht", 7, 1)
-        yh(7, 1)
         store(out_0, "y", 7, 0)
+        yh(7, 1)
         store(out_0, "y", 7, 1)

@@ -43,15 +43,15 @@ def tile_ncpliquidcell_t_kernel(
         nc.vector.memset(zt_bf[:], 0.0)
         zb_bf = const.tile([P, N_HID], BF16)
         nc.vector.memset(zb_bf[:], 0.0)
-        for i, b in enumerate([bg, bh, bfg, bfh]):
-            nc.scalar.dma_start(out=zt_bf[2 * i : 2 * i + 2, :], in_=b.rearrange("(r c) -> r c", r=2))
-        nc.scalar.dma_start(out=zb_bf[0:1, :], in_=bp.rearrange("(o c) -> o c", o=1))
         warm = const.tile([P, 1], F32)
         nc.vector.memset(warm[:], 0.0)
         warm2 = const.tile([P, 1], F32)
         nc.scalar.activation(out=warm2[:], in_=warm[:], func=ACT.Tanh)
         ident = const.tile([P, P], F32)
         make_identity(nc, ident[:])
+        for i, b in enumerate([bg, bh, bfg, bfh]):
+            nc.gpsimd.dma_start(out=zt_bf[2 * i : 2 * i + 2, :], in_=b.rearrange("(r c) -> r c", r=2))
+        nc.gpsimd.dma_start(out=zb_bf[0:1, :], in_=bp.rearrange("(o c) -> o c", o=1))
         ones_bf = const.tile([P, P], BF16)
         nc.vector.memset(ones_bf[:], 1.0)
 
@@ -103,20 +103,24 @@ def tile_ncpliquidcell_t_kernel(
             nc.vector.tensor_copy(out=zt[:], in_=zt_bf[:])
 
         def bt():
-            t["bt"] = tr.tile([P, 512], F32, tag="tr", name="bt")
+            t["bt"] = mx.tile([P, 512], F32, tag="mx", name="bt")
             nc.tensor.transpose(t["bt"][:, 0:P], zt[:], ident[:])
-            t["bb"] = tr.tile([P, 512], F32, tag="tr", name="bb")
+            t["bb"] = mx.tile([P, 512], F32, tag="mx", name="bb")
             nc.tensor.matmul(out=t["bb"][:, 0:N_HID], lhsT=ones_bf[:], rhs=zb_bf[:], start=True, stop=True)
 
         def bv():
             nc.vector.tensor_copy(out=bias_sb[:], in_=t["bt"][:, 0:8])
             nc.vector.tensor_tensor(out=bf_sum[:], in0=bias_sb[:, 4:6], in1=bias_sb[:, 6:8], op=ALU.add)
             nc.vector.tensor_scalar_mul(out=bf_half[:], in0=bf_sum[:], scalar1=0.5)
-            for r in range(2):
-                nc.vector.tensor_copy(out=bp_bc[:, r, :], in_=t["bb"][:, 0:N_HID])
 
-        wc = [const.tile([P, 2, N_HID], U32, name="wc%d" % w, align_bytes=64) for w in range(5)]
-        ws = [const.tile([P, 2, N_HID], U8, name="ws%d" % w, align_bytes=64) for w in range(5)]
+        def bw(eng):
+            for r in range(2):
+                copy_on(eng, bp_bc[:, r, :], t["bb"][:, 0:N_HID])
+
+        wc = [const.tile([P, 2, 2, P], U32, name="wc%d" % w, align_bytes=64) for w in range(4)]
+        ws = [const.tile([P, 2, 2, P], U8, name="ws%d" % w, align_bytes=64) for w in range(4)]
+        wc.append(const.tile([P, 2, N_HID], U32, name="wc4", align_bytes=64))
+        ws.append(const.tile([P, 2, N_HID], U8, name="ws4", align_bytes=64))
 
         def copy_on(eng, out, in_):
             if eng == "S":
@@ -136,18 +140,25 @@ def tile_ncpliquidcell_t_kernel(
 
         def wcp(w, hf, eng):
             if ("wg", w) not in t:
-                t["wg", w] = wgr.tile([P, 2, N_HID, 2], F32, tag="wg", name="wg", align_bytes=64)
-            copy_on(
-                eng,
-                t["wg", w][:, :, P * hf : P * (hf + 1), :],
-                t["wt", w, hf][:].rearrange("q (g u c) -> q g c u", g=2, u=2),
-            )
+                t["wg", w] = wgr.tile([P, 2, 2, P, 2], F32, tag="wg", name="wg", align_bytes=64)
+            if w < 4:
+                dst = t["wg", w][:, hf, :, :, :]
+            else:
+                dst = t["wg", w][:].rearrange("q a b c u -> q a (b c) u")[:, :, P * hf : P * (hf + 1), :]
+            copy_on(eng, dst, t["wt", w, hf][:].rearrange("q (g u c) -> q g c u", g=2, u=2))
 
         def wq(w):
             nc.vector.quantize_mx(
                 out=wc[w][:].rearrange("q g c -> q (g c)").bitcast(FP8X4),
                 scales=ws[w][:].rearrange("q g c -> q (g c)"),
-                in_=t["wg", w][:].rearrange("q g c u -> q (g c u)").bitcast(BF16),
+                in_=t["wg", w][:].rearrange("q a b c u -> q (a b c u)").bitcast(BF16),
+            )
+
+        def wh(w, hf):
+            nc.vector.quantize_mx(
+                out=wc[w][:, hf, :, :].rearrange("q g c -> q (g c)").bitcast(FP8X4),
+                scales=ws[w][:, hf, :, :].rearrange("q g c -> q (g c)"),
+                in_=t["wg", w][:, hf, :, :, :].rearrange("q g c u -> q (g c u)").bitcast(BF16),
             )
 
         def xt(s, j):
@@ -181,7 +192,6 @@ def tile_ncpliquidcell_t_kernel(
         def mxl(s, lay, hf):
             acc = mx.tile([P, 512], F32, tag="mx", name="acc")
             t["acc", s, lay, hf] = acc
-            cols = slice(P * hf, P * (hf + 1))
             wlist = layers[lay]
             n = 2 * len(wlist)
             i = 0
@@ -189,8 +199,8 @@ def tile_ncpliquidcell_t_kernel(
                 for g in range(2):
                     nc.tensor.matmul_mx(
                         out=acc[:],
-                        lhsT=wc[w][:, g, cols].bitcast(FP8X4),
-                        lhsT_scale=ws[w][:, g, cols],
+                        lhsT=wc[w][:, hf, g, :].bitcast(FP8X4),
+                        lhsT_scale=ws[w][:, hf, g, :],
                         rhs=t["xc", s][:, g, :].bitcast(FP8X4),
                         rhs_scale=t["xs", s][:, g, :],
                         start=(i == 0),
@@ -307,92 +317,97 @@ def tile_ncpliquidcell_t_kernel(
             else:
                 nc.sync.dma_start(out=view[:, 2 * jp : 2 * jp + 2, :], in_=t[key, s][:, 2 * jp : 2 * jp + 2, :])
 
-        bc()
-        bt()
-        bv()
-        xt(0, 0)
         xt(0, 1)
-        xt(0, 3)
-        xcp(0, 1, "S")
-        xcp(0, 0, "V")
         mm(0, 0)
-        mm(0, 1)
         xt(0, 2)
-        wt(0, 0)
-        wt(0, 1)
-        xcp(0, 3, "S")
+        xt(0, 3)
+        xt(0, 0)
+        xcp(0, 2, "S")
+        mm(0, 1)
+        xcp(0, 1, "S")
         mm(1, 0)
         mm(1, 1)
+        xcp(0, 3, "S")
+        wt(0, 0)
         wcp(0, 0, "S")
-        xcp(0, 2, "S")
-        wcp(0, 1, "S")
+        wt(0, 1)
+        xcp(0, 0, "S")
+        wh(0, 0)
         wt(1, 0)
+        bc()
         wt(1, 1)
-        wcp(1, 1, "S")
         xqz(0)
-        wq(0)
-        mm(2, 0)
-        xt(1, 3)
         wcp(1, 0, "S")
-        wq(1)
+        wcp(1, 1, "S")
+        wh(1, 0)
+        bt()
+        wcp(0, 1, "S")
+        wh(0, 1)
+        bv()
+        mxl(0, "g", 0)
+        mm(2, 0)
+        mm(3, 0)
+        actl(0, "g", 0)
+        xt(1, 3)
+        xcp(1, 3, "S")
+        bw("S")
+        wh(1, 1)
         mm(2, 1)
         mxl(0, "g", 1)
-        xcp(1, 3, "S")
-        actl(0, "g", 1)
         wt(2, 0)
-        mxl(0, "h", 1)
-        mxl(0, "g", 0)
-        actl(0, "h", 1)
-        mm(3, 1)
-        wt(3, 1)
-        mm(3, 0)
         wcp(2, 0, "S")
-        mm(4, 0)
-        xt(1, 1)
-        mm(4, 1)
-        wcp(3, 1, "S")
-        actl(0, "g", 0)
-        wt(2, 1)
-        wcp(2, 1, "S")
         wt(3, 0)
+        xt(1, 1)
+        mxl(0, "h", 1)
+        wcp(3, 0, "S")
+        mm(3, 1)
+        wt(2, 1)
+        mm(4, 1)
+        wh(2, 0)
+        wt(3, 1)
         xcp(1, 1, "V")
-        mxl(0, "h", 0)
-        xt(1, 2)
-        wcp(3, 0, "V")
+        actl(0, "g", 1)
+        mm(4, 0)
         xt(1, 0)
-        wq(2)
+        wcp(2, 1, "S")
+        wcp(3, 1, "S")
+        wh(2, 1)
+        wh(3, 0)
+        mxl(0, "h", 0)
         wt(4, 1)
-        wq(3)
-        wt(4, 0)
-        actl(0, "h", 0)
+        actl(0, "h", 1)
         wcp(4, 1, "S")
-        wcp(4, 0, "S")
-        xcp(1, 0, "S")
+        wt(4, 0)
+        xt(1, 2)
+        wh(3, 1)
+        wcp(4, 0, "V")
         mxl(0, "f", 0)
-        dd(0, 0)
         mxl(0, "f", 1)
+        actl(0, "h", 0)
+        dd(0, 1)
+        xcp(1, 0, "S")
         wq(4)
         mxp(0, 0)
-        actl(0, "f", 0)
-        dd(0, 1)
         xcp(1, 2, "S")
-        ee(0, 0)
+        dd(0, 0)
         actl(0, "f", 1)
         xqz(1)
-        nn(0, 0)
-        mxp(0, 1)
-        pbias(0, 0)
+        actl(0, "f", 0)
+        xt(2, 3)
+        xt(2, 2)
         xt(2, 0)
         ee(0, 1)
-        xt(2, 1)
-        xcp(2, 0, "S")
-        xt(2, 3)
+        ee(0, 0)
         xcp(2, 3, "S")
-        xcp(2, 1, "S")
-        pbias(0, 1)
-        xt(2, 2)
-        nn(0, 1)
+        xt(2, 1)
+        mxp(0, 1)
+        pbias(0, 0)
+        nn(0, 0)
+        xcp(2, 0, "S")
         xcp(2, 2, "S")
+        pbias(0, 1)
+        nn(0, 1)
+        xcp(2, 1, "S")
         mxl(1, "g", 0)
         mxl(1, "h", 0)
         mxl(1, "f", 0)

@@ -32,13 +32,17 @@ def tile_ncpliquidcell_t_kernel(
         xin = ctx.enter_context(tc.tile_pool(name="xin", bufs=NSB))
         xgr = ctx.enter_context(tc.tile_pool(name="xgr", bufs=2))
         xq = ctx.enter_context(tc.tile_pool(name="xq", bufs=3))
-        act = ctx.enter_context(tc.tile_pool(name="act", bufs=2))
+        act = ctx.enter_context(tc.tile_pool(name="act", bufs=3))
         ep = ctx.enter_context(tc.tile_pool(name="ep", bufs=2))
         outp = ctx.enter_context(tc.tile_pool(name="outp", bufs=3))
         tr = ctx.enter_context(tc.psum_pool(name="tr", bufs=4))
         mx = ctx.enter_context(tc.psum_pool(name="mx", bufs=4))
         ctx.enter_context(tc.manual_schedule())
 
+        ones_bf = const.tile([P, P], BF16)
+        nc.vector.memset(ones_bf[:], 1.0)
+        dz = const.tile([P, 512], BF16)
+        nc.vector.memset(dz[:], 0.0)
         zt_bf = const.tile([P, P], BF16)
         nc.vector.memset(zt_bf[:], 0.0)
         zb_bf = const.tile([P, N_HID], BF16)
@@ -52,8 +56,6 @@ def tile_ncpliquidcell_t_kernel(
         for i, b in enumerate([bg, bh, bfg, bfh]):
             nc.gpsimd.dma_start(out=zt_bf[2 * i : 2 * i + 2, :], in_=b.rearrange("(r c) -> r c", r=2))
         nc.gpsimd.dma_start(out=zb_bf[0:1, :], in_=bp.rearrange("(o c) -> o c", o=1))
-        ones_bf = const.tile([P, P], BF16)
-        nc.vector.memset(ones_bf[:], 1.0)
 
         mask_sb = [const.tile([P, K], BF16, name="mask%d" % hf) for hf in range(2)]
         w_sb = [[wraw.tile([P, K], BF16, name="w%d_%d" % (w, hf), tag="w") for hf in range(2)] for w in range(5)]
@@ -98,6 +100,11 @@ def tile_ncpliquidcell_t_kernel(
         bf_half = const.tile([P, 2], F32)
         bp_bc = const.tile([P, 2, N_HID], F32)
         t = {}
+
+        def dm():
+            if "dm" not in t:
+                t["dm"] = mx.tile([P, 512], F32, tag="mx", name="dmb")
+            nc.tensor.matmul(out=t["dm"][:], lhsT=ones_bf[:], rhs=dz[:], start=True, stop=True)
 
         def bc():
             nc.vector.tensor_copy(out=zt[:], in_=zt_bf[:])
@@ -317,135 +324,147 @@ def tile_ncpliquidcell_t_kernel(
             else:
                 nc.sync.dma_start(out=view[:, 2 * jp : 2 * jp + 2, :], in_=t[key, s][:, 2 * jp : 2 * jp + 2, :])
 
-        xt(0, 1)
+        dm()
         mm(0, 0)
-        xt(0, 2)
+        dm()
+        dm()
+        dm()
+        dm()
+        dm()
+        dm()
+        dm()
+        xt(0, 1)
         xt(0, 3)
-        xt(0, 0)
-        xcp(0, 2, "S")
         mm(0, 1)
         xcp(0, 1, "S")
         mm(1, 0)
-        mm(1, 1)
-        xcp(0, 3, "S")
-        wt(0, 0)
-        wcp(0, 0, "S")
-        wt(0, 1)
+        xt(0, 2)
+        xt(0, 0)
+        xcp(0, 2, "S")
+        dm()
+        dm()
         xcp(0, 0, "S")
-        wh(0, 0)
-        wt(1, 0)
-        bc()
-        wt(1, 1)
-        xqz(0)
-        wcp(1, 0, "S")
-        wcp(1, 1, "S")
-        wh(1, 0)
-        bt()
+        xcp(0, 3, "S")
+        wt(0, 1)
         wcp(0, 1, "S")
+        xqz(0)
+        dm()
+        dm()
+        wt(1, 0)
+        wt(0, 0)
         wh(0, 1)
-        bv()
-        mxl(0, "g", 0)
-        mm(2, 0)
-        mm(3, 0)
-        actl(0, "g", 0)
-        xt(1, 3)
-        xcp(1, 3, "S")
-        bw("S")
-        wh(1, 1)
-        mm(2, 1)
         mxl(0, "g", 1)
-        wt(2, 0)
-        wcp(2, 0, "S")
-        wt(3, 0)
-        xt(1, 1)
-        mxl(0, "h", 1)
-        wcp(3, 0, "S")
-        mm(3, 1)
-        wt(2, 1)
-        mm(4, 1)
-        wh(2, 0)
-        wt(3, 1)
-        xcp(1, 1, "V")
-        actl(0, "g", 1)
-        mm(4, 0)
-        xt(1, 0)
-        wcp(2, 1, "S")
-        wcp(3, 1, "S")
-        wh(2, 1)
-        wh(3, 0)
-        mxl(0, "h", 0)
-        wt(4, 1)
-        actl(0, "h", 1)
-        wcp(4, 1, "S")
-        wt(4, 0)
+        mm(1, 1)
+        wcp(1, 0, "S")
+        wt(1, 1)
+        wcp(0, 0, "S")
+        wh(1, 0)
+        wcp(1, 1, "S")
+        bc()
         xt(1, 2)
-        wh(3, 1)
-        wcp(4, 0, "V")
-        mxl(0, "f", 0)
-        mxl(0, "f", 1)
-        actl(0, "h", 0)
-        dd(0, 1)
-        xcp(1, 0, "S")
-        wq(4)
-        mxp(0, 0)
+        bt()
+        xt(1, 3)
+        wh(0, 0)
         xcp(1, 2, "S")
-        dd(0, 0)
-        actl(0, "f", 1)
+        mm(2, 0)
+        bv()
+        xcp(1, 3, "V")
+        mxl(0, "g", 0)
+        wh(1, 1)
+        actl(0, "g", 1)
+        xt(1, 1)
+        xt(1, 0)
+        mm(2, 1)
+        bw("S")
+        mxl(0, "h", 1)
+        mxl(0, "h", 0)
+        xcp(1, 0, "S")
+        mm(3, 1)
+        wt(2, 0)
+        wt(3, 1)
+        mm(3, 0)
+        xcp(1, 1, "S")
+        wt(3, 0)
+        actl(0, "g", 0)
+        actl(0, "h", 0)
         xqz(1)
-        actl(0, "f", 0)
-        xt(2, 3)
-        xt(2, 2)
-        xt(2, 0)
-        ee(0, 1)
-        ee(0, 0)
-        xcp(2, 3, "S")
-        xt(2, 1)
-        mxp(0, 1)
-        pbias(0, 0)
-        nn(0, 0)
-        xcp(2, 0, "S")
-        xcp(2, 2, "S")
-        pbias(0, 1)
-        nn(0, 1)
-        xcp(2, 1, "S")
+        actl(0, "h", 1)
+        wt(2, 1)
+        wcp(3, 0, "V")
+        wcp(3, 1, "V")
+        wh(3, 0)
         mxl(1, "g", 0)
-        mxl(1, "h", 0)
-        mxl(1, "f", 0)
+        mxl(1, "h", 1)
+        wcp(2, 0, "S")
+        mxl(1, "g", 1)
         actl(1, "g", 0)
-        nt(0, 0)
-        nt(0, 1)
-        xt(3, 0)
-        xqz(2)
+        wh(3, 1)
+        wh(2, 0)
+        mxl(1, "h", 0)
+        dd(0, 0)
+        wcp(2, 1, "S")
+        wh(2, 1)
+        actl(1, "h", 1)
+        mm(4, 1)
+        mm(4, 0)
+        actl(1, "g", 1)
         actl(1, "h", 0)
         dd(1, 0)
-        actl(1, "f", 0)
-        mxl(1, "g", 1)
-        mxl(1, "h", 1)
-        ee(1, 0)
-        ncp(0, 0, "S")
+        mxl(0, "f", 0)
+        actl(0, "f", 0)
+        ee(0, 0)
+        dd(0, 1)
+        nn(0, 0)
+        mxl(0, "f", 1)
+        wt(4, 0)
+        wt(4, 1)
+        xt(2, 0)
+        xt(2, 1)
+        mxl(1, "f", 0)
+        wcp(4, 0, "S")
+        actl(0, "f", 1)
+        wcp(4, 1, "S")
         mxl(1, "f", 1)
+        xcp(2, 1, "S")
+        xcp(2, 0, "S")
+        xt(2, 3)
+        xt(2, 2)
+        actl(1, "f", 0)
+        ee(0, 1)
+        dd(1, 1)
+        nn(0, 1)
+        nt(0, 1)
+        wq(4)
+        nt(0, 0)
+        mxp(0, 0)
+        ee(1, 0)
+        actl(1, "f", 1)
         mxp(1, 0)
-        ncp(0, 1, "S")
+        ee(1, 1)
         nn(1, 0)
-        xcp(3, 0, "S")
-        actl(1, "g", 1)
+        ncp(0, 0, "S")
+        ncp(0, 1, "S")
+        pbias(0, 0)
+        mxp(1, 1)
+        xcp(2, 2, "S")
+        mxp(0, 1)
+        nn(1, 1)
+        xcp(2, 3, "S")
+        pbias(1, 0)
+        xt(3, 1)
+        xt(3, 0)
+        xqz(2)
+        xt(3, 2)
+        xt(3, 3)
+        pbias(0, 1)
+        pbias(1, 1)
         yy(0)
-        actl(1, "h", 1)
+        xcp(3, 0, "S")
+        xcp(3, 3, "S")
         store(out_1, "nht", 0, None)
         store(out_0, "y", 0, None)
-        mxp(1, 1)
-        dd(1, 1)
-        xt(3, 1)
-        actl(1, "f", 1)
         xcp(3, 1, "S")
-        xt(3, 2)
-        pbias(1, 0)
-        ee(1, 1)
-        xt(3, 3)
-        pbias(1, 1)
         xcp(3, 2, "S")
-        nn(1, 1)
-        xcp(3, 3, "S")
         mxl(2, "g", 0)
         mxl(2, "h", 0)
         mxl(2, "f", 0)

from contextlib import ExitStack

import concourse.mybir as mybir
from concourse.masks import make_identity

F32 = mybir.dt.float32
BF16 = mybir.dt.bfloat16
U32 = mybir.dt.uint32
U8 = mybir.dt.uint8
FP8X4 = mybir.dt.float8_e4m3fn_x4
ALU = mybir.AluOpType
ACT = mybir.ActivationFunctionType

P = 128
B, IN_F, N_HID = 4096, 768, 256
K = IN_F + N_HID
SB = 512
JT = SB // P
NSB = B // SB
FLOPS = 2 * B * K * 5 * N_HID


def tile_ncpliquidcell_t_kernel(
    tc, x, hidden, mask, Wg, bg, Wh, bh, Wfg, bfg, Wfh, bfh, Wp, bp, out_0, out_1
):
    nc = tc.nc
    weights = [Wg, Wh, Wfg, Wfh, Wp]
    with ExitStack() as ctx:
        const = ctx.enter_context(tc.tile_pool(name="const", bufs=1))
        wraw = ctx.enter_context(tc.tile_pool(name="wraw", bufs=10))
        wgr = ctx.enter_context(tc.tile_pool(name="wgr", bufs=2))
        xin = ctx.enter_context(tc.tile_pool(name="xin", bufs=NSB))
        xgr = ctx.enter_context(tc.tile_pool(name="xgr", bufs=2))
        xq = ctx.enter_context(tc.tile_pool(name="xq", bufs=3))
        act = ctx.enter_context(tc.tile_pool(name="act", bufs=3))
        ep = ctx.enter_context(tc.tile_pool(name="ep", bufs=2))
        outp = ctx.enter_context(tc.tile_pool(name="outp", bufs=3))
        tr = ctx.enter_context(tc.psum_pool(name="tr", bufs=4))
        mx = ctx.enter_context(tc.psum_pool(name="mx", bufs=4))
        ctx.enter_context(tc.manual_schedule())

        ones_bf = const.tile([P, P], BF16)
        nc.vector.memset(ones_bf[:], 1.0)
        dz = const.tile([P, 512], BF16)
        nc.vector.memset(dz[:], 0.0)
        zt_bf = const.tile([P, P], BF16)
        nc.vector.memset(zt_bf[:], 0.0)
        zb_bf = const.tile([P, N_HID], BF16)
        nc.vector.memset(zb_bf[:], 0.0)
        warm = const.tile([P, 1], F32)
        nc.vector.memset(warm[:], 0.0)
        warm2 = const.tile([P, 1], F32)
        nc.scalar.activation(out=warm2[:], in_=warm[:], func=ACT.Tanh)
        ident = const.tile([P, P], F32)
        make_identity(nc, ident[:])
        for i, b in enumerate([bg, bh, bfg, bfh]):
            nc.gpsimd.dma_start(out=zt_bf[2 * i : 2 * i + 2, :], in_=b.rearrange("(r c) -> r c", r=2))
        nc.gpsimd.dma_start(out=zb_bf[0:1, :], in_=bp.rearrange("(o c) -> o c", o=1))

        mask_sb = [const.tile([P, K], BF16, name="mask%d" % hf) for hf in range(2)]
        w_sb = [[wraw.tile([P, K], BF16, name="w%d_%d" % (w, hf), tag="w") for hf in range(2)] for w in range(5)]
        x_sb = [xin.tile([P, JT, IN_F], BF16, name="x%d" % s, tag="x") for s in range(NSB)]
        h_sb = [xin.tile([P, JT, N_HID], BF16, name="h%d" % s, tag="h") for s in range(NSB)]

        def load_m(hf):
            nc.sync.dma_start(out=mask_sb[hf][:], in_=mask[P * hf : P * (hf + 1), :])

        def load_w(w, hf):
            nc.sync.dma_start(out=w_sb[w][hf][:], in_=weights[w][P * hf : P * (hf + 1), :])

        def load_x(s):
            rows = slice(SB * s, SB * (s + 1))
            nc.sync.dma_start(out=x_sb[s][:], in_=x[rows, :].rearrange("(p j) k -> p j k", j=JT))
            nc.sync.dma_start(out=h_sb[s][:], in_=hidden[rows, :].rearrange("(p j) k -> p j k", j=JT))

        load_x(0)
        load_m(0)
        load_w(0, 0)
        load_m(1)
        load_w(0, 1)
        load_w(1, 0)
        load_w(1, 1)
        load_x(1)
        load_w(2, 0)
        load_w(2, 1)
        load_w(3, 0)
        load_w(3, 1)
        load_w(4, 0)
        load_w(4, 1)
        load_x(2)
        load_x(3)
        load_x(4)
        load_x(5)
        load_x(6)
        load_x(7)

        zt = const.tile([P, P], F32)
        bias_sb = const.tile([P, 8], F32)
        bf_sum = const.tile([P, 2], F32)
        bf_half = const.tile([P, 2], F32)
        bp_bc = const.tile([P, 2, N_HID], F32)
        t = {}

        def dm():
            if "dm" not in t:
                t["dm"] = mx.tile([P, 512], F32, tag="mx", name="dmb")
            nc.tensor.matmul(out=t["dm"][:], lhsT=ones_bf[:], rhs=dz[:], start=True, stop=True)

        def bc():
            nc.vector.tensor_copy(out=zt[:], in_=zt_bf[:])

        def bt():
            t["bt"] = mx.tile([P, 512], F32, tag="mx", name="bt")
            nc.tensor.transpose(t["bt"][:, 0:P], zt[:], ident[:])
            t["bb"] = mx.tile([P, 512], F32, tag="mx", name="bb")
            nc.tensor.matmul(out=t["bb"][:, 0:N_HID], lhsT=ones_bf[:], rhs=zb_bf[:], start=True, stop=True)

        def bv():
            nc.vector.tensor_copy(out=bias_sb[:], in_=t["bt"][:, 0:8])
            nc.vector.tensor_tensor(out=bf_sum[:], in0=bias_sb[:, 4:6], in1=bias_sb[:, 6:8], op=ALU.add)
            nc.vector.tensor_scalar_mul(out=bf_half[:], in0=bf_sum[:], scalar1=0.5)

        def bw(eng):
            for r in range(2):
                copy_on(eng, bp_bc[:, r, :], t["bb"][:, 0:N_HID])

        wc = [const.tile([P, 2, 2, P], U32, name="wc%d" % w, align_bytes=64) for w in range(4)]
        ws = [const.tile([P, 2, 2, P], U8, name="ws%d" % w, align_bytes=64) for w in range(4)]
        wc.append(const.tile([P, 2, N_HID], U32, name="wc4", align_bytes=64))
        ws.append(const.tile([P, 2, N_HID], U8, name="ws4", align_bytes=64))

        def copy_on(eng, out, in_):
            if eng == "S":
                nc.scalar.copy(out=out, in_=in_)
            else:
                nc.vector.tensor_copy(out=out, in_=in_)

        def mm(w, hf):
            nc.vector.tensor_tensor(out=w_sb[w][hf][:], in0=w_sb[w][hf][:], in1=mask_sb[hf][:], op=ALU.mult)

        def wt(w, hf):
            bank = tr.tile([P, 512], F32, tag="tr", name="wt")
            t["wt", w, hf] = bank
            ww = w_sb[w][hf][:].bitcast(F32)
            for b in range(4):
                nc.tensor.transpose(bank[:, P * b : P * (b + 1)], ww[:, P * b : P * (b + 1)], ident[:])

        def wcp(w, hf, eng):
            if ("wg", w) not in t:
                t["wg", w] = wgr.tile([P, 2, 2, P, 2], F32, tag="wg", name="wg", align_bytes=64)
            if w < 4:
                dst = t["wg", w][:, hf, :, :, :]
            else:
                dst = t["wg", w][:].rearrange("q a b c u -> q a (b c) u")[:, :, P * hf : P * (hf + 1), :]
            copy_on(eng, dst, t["wt", w, hf][:].rearrange("q (g u c) -> q g c u", g=2, u=2))

        def wq(w):
            nc.vector.quantize_mx(
                out=wc[w][:].rearrange("q g c -> q (g c)").bitcast(FP8X4),
                scales=ws[w][:].rearrange("q g c -> q (g c)"),
                in_=t["wg", w][:].rearrange("q a b c u -> q (a b c u)").bitcast(BF16),
            )

        def wh(w, hf):
            nc.vector.quantize_mx(
                out=wc[w][:, hf, :, :].rearrange("q g c -> q (g c)").bitcast(FP8X4),
                scales=ws[w][:, hf, :, :].rearrange("q g c -> q (g c)"),
                in_=t["wg", w][:, hf, :, :, :].rearrange("q g c u -> q (g c u)").bitcast(BF16),
            )

        def xt(s, j):
            bank = tr.tile([P, 512], F32, tag="tr", name="xt")
            t["xt", s, j] = bank
            xw = x_sb[s][:, j, :].bitcast(F32)
            for b in range(3):
                nc.tensor.transpose(bank[:, P * b : P * (b + 1)], xw[:, P * b : P * (b + 1)], ident[:])
            nc.tensor.transpose(bank[:, 3 * P : 4 * P], h_sb[s][:, j, :].bitcast(F32), ident[:])

        def xcp(s, j, eng):
            if ("xg", s) not in t:
                t["xg", s] = xgr.tile([P, 2, SB, 2], F32, tag="xg", name="xg", align_bytes=64)
            copy_on(
                eng,
                t["xg", s][:, :, P * j : P * (j + 1), :],
                t["xt", s, j][:].rearrange("q (g u c) -> q g c u", g=2, u=2),
            )

        def xqz(s):
            t["xc", s] = xq.tile([P, 2, SB], U32, tag="xc", name="xc", align_bytes=64)
            t["xs", s] = xq.tile([P, 2, SB], U8, tag="xs", name="xs", align_bytes=64)
            nc.vector.quantize_mx(
                out=t["xc", s][:].rearrange("q g c -> q (g c)").bitcast(FP8X4),
                scales=t["xs", s][:].rearrange("q g c -> q (g c)"),
                in_=t["xg", s][:].rearrange("q g c u -> q (g c u)").bitcast(BF16),
            )

        layers = {"g": [0], "h": [1], "f": [2, 3]}

        def mxl(s, lay, hf):
            acc = mx.tile([P, 512], F32, tag="mx", name="acc")
            t["acc", s, lay, hf] = acc
            wlist = layers[lay]
            n = 2 * len(wlist)
            i = 0
            for w in wlist:
                for g in range(2):
                    nc.tensor.matmul_mx(
                        out=acc[:],
                        lhsT=wc[w][:, hf, g, :].bitcast(FP8X4),
                        lhsT_scale=ws[w][:, hf, g, :],
                        rhs=t["xc", s][:, g, :].bitcast(FP8X4),
                        rhs_scale=t["xs", s][:, g, :],
                        start=(i == 0),
                        stop=(i == n - 1),
                    )
                    i += 1

        def actl(s, lay, hf):
            if (lay, s) not in t:
                t[lay, s] = act.tile([P, 2, SB], F32, tag=lay, name="a" + lay)
            if lay == "g":
                bias, scale = bias_sb[:, hf : hf + 1], 1.0
            elif lay == "h":
                bias, scale = bias_sb[:, 2 + hf : 3 + hf], 1.0
            else:
                bias, scale = bf_half[:, hf : hf + 1], 0.5
            nc.scalar.activation(out=t[lay, s][:, hf, :], in_=t["acc", s, lay, hf][:], func=ACT.Tanh, bias=bias, scale=scale)

        def actf2(s, k):
            hf, c = k // 2, k % 2
            cols = slice(N_HID * c, N_HID * (c + 1))
            if ("f", s) not in t:
                t["f", s] = act.tile([P, 2, SB], F32, tag="f", name="af")
            nc.scalar.activation(
                out=t["f", s][:, hf, cols], in_=t["acc", s, "f", hf][:, cols], func=ACT.Tanh, bias=bf_half[:, hf : hf + 1], scale=0.5
            )

        def ee2(s, k):
            hf, c = k // 2, k % 2
            cols = slice(N_HID * c, N_HID * (c + 1))
            nc.vector.scalar_tensor_tensor(
                out=t["d", s][:, hf, cols], in0=t["f", s][:, hf, cols], scalar=1.0, in1=t["d", s][:, hf, cols], op0=ALU.add, op1=ALU.mult
            )

        def nn2(s, k):
            hf, c = k // 2, k % 2
            cols = slice(N_HID * c, N_HID * (c + 1))
            if ("nh", s) not in t:
                t["nh", s] = ep.tile([P, 2, SB], F32, tag="nh", name="nh")
            nc.vector.scalar_tensor_tensor(
                out=t["nh", s][:, hf, cols], in0=t["d", s][:, hf, cols], scalar=0.5, in1=t["g", s][:, hf, cols], op0=ALU.mult, op1=ALU.add
            )

        def mxp(s, jp):
            acc = mx.tile([P, 512], F32, tag="mx", name="accp")
            t["accp", s, jp] = acc
            for jj in range(2):
                cols = slice(P * (2 * jp + jj), P * (2 * jp + jj + 1))
                for g in range(2):
                    nc.tensor.matmul_mx(
                        out=acc[:, N_HID * jj : N_HID * (jj + 1)],
                        lhsT=t["xc", s][:, g, cols].bitcast(FP8X4),
                        lhsT_scale=t["xs", s][:, g, cols],
                        rhs=wc[4][:, g, :].bitcast(FP8X4),
                        rhs_scale=ws[4][:, g, :],
                        start=(g == 0),
                        stop=(g == 1),
                    )

        def half(tile_, jp):
            return tile_[:, 2 * jp : 2 * jp + 2, :].rearrange("p a f -> p (a f)")

        def pbias(s, jp):
            if ("pb", s) not in t:
                t["pb", s] = outp.tile([P, JT, N_HID], F32, tag="pb", name="pb")
            nc.vector.tensor_tensor(
                out=half(t["pb", s], jp), in0=t["accp", s, jp][:], in1=bp_bc[:].rearrange("p a f -> p (a f)"), op=ALU.add
            )

        def dd(s, hf):
            if ("d", s) not in t:
                t["d", s] = ep.tile([P, 2, SB], F32, tag="d", name="d")
            nc.vector.tensor_tensor(out=t["d", s][:, hf, :], in0=t["h", s][:, hf, :], in1=t["g", s][:, hf, :], op=ALU.subtract)

        def ee(s, hf):
            nc.vector.scalar_tensor_tensor(
                out=t["d", s][:, hf, :], in0=t["f", s][:, hf, :], scalar=1.0, in1=t["d", s][:, hf, :], op0=ALU.add, op1=ALU.mult
            )

        def nn(s, hf):
            if ("nh", s) not in t:
                t["nh", s] = ep.tile([P, 2, SB], F32, tag="nh", name="nh")
            nc.vector.scalar_tensor_tensor(
                out=t["nh", s][:, hf, :], in0=t["d", s][:, hf, :], scalar=0.5, in1=t["g", s][:, hf, :], op0=ALU.mult, op1=ALU.add
            )

        def nt(s, jp):
            bank = tr.tile([P, 512], F32, tag="tr", name="nt")
            t["nt", s, jp] = bank
            for jj in range(2):
                j = 2 * jp + jj
                for hf in range(2):
                    o = N_HID * jj + P * hf
                    nc.tensor.transpose(bank[:, o : o + P], t["nh", s][:, hf, P * j : P * (j + 1)], ident[:])

        def ncp(s, jp, eng):
            if ("nht", s) not in t:
                t["nht", s] = outp.tile([P, JT, N_HID], F32, tag="nht", name="nht")
            copy_on(eng, half(t["nht", s], jp), t["nt", s, jp][:])

        def yh(s, jp):
            if ("y", s) not in t:
                t["y", s] = outp.tile([P, JT, N_HID], F32, tag="y", name="y")
            nc.vector.tensor_tensor(out=half(t["y", s], jp), in0=half(t["nht", s], jp), in1=half(t["pb", s], jp), op=ALU.add)

        def yy(s):
            t["y", s] = outp.tile([P, JT, N_HID], F32, tag="y", name="y")
            nc.vector.tensor_tensor(out=t["y", s][:], in0=t["nht", s][:], in1=t["pb", s][:], op=ALU.add)

        def store(dst, key, s, jp):
            view = dst[SB * s : SB * (s + 1), :].rearrange("(p j) f -> p j f", j=JT)
            if jp is None:
                nc.sync.dma_start(out=view, in_=t[key, s][:])
            else:
                nc.sync.dma_start(out=view[:, 2 * jp : 2 * jp + 2, :], in_=t[key, s][:, 2 * jp : 2 * jp + 2, :])

        dm()
        mm(0, 0)
        dm()
        dm()
        dm()
        dm()
        dm()
        dm()
        dm()
        xt(0, 1)
        xt(0, 3)
        mm(0, 1)
        xcp(0, 1, "S")
        mm(1, 0)
        xt(0, 2)
        xt(0, 0)
        xcp(0, 2, "S")
        dm()
        dm()
        xcp(0, 0, "S")
        xcp(0, 3, "S")
        wt(0, 1)
        wcp(0, 1, "S")
        xqz(0)
        dm()
        dm()
        wt(1, 0)
        wt(0, 0)
        wh(0, 1)
        mxl(0, "g", 1)
        mm(1, 1)
        wcp(1, 0, "S")
        wt(1, 1)
        wcp(0, 0, "S")
        wh(1, 0)
        wcp(1, 1, "S")
        bc()
        xt(1, 2)
        bt()
        xt(1, 3)
        wh(0, 0)
        xcp(1, 2, "S")
        mm(2, 0)
        bv()
        xcp(1, 3, "V")
        mxl(0, "g", 0)
        wh(1, 1)
        actl(0, "g", 1)
        xt(1, 1)
        xt(1, 0)
        mm(2, 1)
        bw("S")
        mxl(0, "h", 1)
        mxl(0, "h", 0)
        xcp(1, 0, "S")
        mm(3, 1)
        wt(2, 0)
        wt(3, 1)
        mm(3, 0)
        xcp(1, 1, "S")
        wt(3, 0)
        actl(0, "g", 0)
        actl(0, "h", 0)
        xqz(1)
        actl(0, "h", 1)
        wt(2, 1)
        wcp(3, 0, "V")
        wcp(3, 1, "V")
        wh(3, 0)
        mxl(1, "g", 0)
        mxl(1, "h", 1)
        wcp(2, 0, "S")
        mxl(1, "g", 1)
        actl(1, "g", 0)
        wh(3, 1)
        wh(2, 0)
        mxl(1, "h", 0)
        dd(0, 0)
        wcp(2, 1, "S")
        wh(2, 1)
        actl(1, "h", 1)
        mm(4, 1)
        mm(4, 0)
        actl(1, "g", 1)
        actl(1, "h", 0)
        dd(1, 0)
        mxl(0, "f", 0)
        actl(0, "f", 0)
        ee(0, 0)
        dd(0, 1)
        nn(0, 0)
        mxl(0, "f", 1)
        wt(4, 0)
        wt(4, 1)
        xt(2, 0)
        xt(2, 1)
        mxl(1, "f", 0)
        wcp(4, 0, "S")
        actl(0, "f", 1)
        wcp(4, 1, "S")
        mxl(1, "f", 1)
        xcp(2, 1, "S")
        xcp(2, 0, "S")
        xt(2, 3)
        xt(2, 2)
        actl(1, "f", 0)
        ee(0, 1)
        dd(1, 1)
        nn(0, 1)
        nt(0, 1)
        wq(4)
        nt(0, 0)
        mxp(0, 0)
        ee(1, 0)
        actl(1, "f", 1)
        mxp(1, 0)
        ee(1, 1)
        nn(1, 0)
        ncp(0, 0, "S")
        ncp(0, 1, "S")
        pbias(0, 0)
        mxp(1, 1)
        xcp(2, 2, "S")
        mxp(0, 1)
        nn(1, 1)
        xcp(2, 3, "S")
        pbias(1, 0)
        xt(3, 1)
        xt(3, 0)
        xqz(2)
        xt(3, 2)
        xt(3, 3)
        pbias(0, 1)
        pbias(1, 1)
        yy(0)
        xcp(3, 0, "S")
        xcp(3, 3, "S")
        store(out_1, "nht", 0, None)
        store(out_0, "y", 0, None)
        xcp(3, 1, "S")
        xcp(3, 2, "S")
        mxl(2, "g", 0)
        mxl(2, "h", 0)
        mxl(2, "f", 0)
        actl(2, "g", 0)
        nt(1, 0)
        nt(1, 1)
        xt(4, 0)
        xqz(3)
        actl(2, "h", 0)
        dd(2, 0)
        actl(2, "f", 0)
        mxl(2, "g", 1)
        mxl(2, "h", 1)
        ee(2, 0)
        ncp(1, 0, "S")
        mxl(2, "f", 1)
        mxp(2, 0)
        ncp(1, 1, "S")
        nn(2, 0)
        xcp(4, 0, "S")
        actl(2, "g", 1)
        yy(1)
        actl(2, "h", 1)
        store(out_1, "nht", 1, None)
        store(out_0, "y", 1, None)
        mxp(2, 1)
        dd(2, 1)
        xt(4, 1)
        actl(2, "f", 1)
        xcp(4, 1, "S")
        xt(4, 2)
        pbias(2, 0)
        ee(2, 1)
        xt(4, 3)
        pbias(2, 1)
        xcp(4, 2, "S")
        nn(2, 1)
        xcp(4, 3, "S")
        mxl(3, "g", 0)
        mxl(3, "h", 0)
        mxl(3, "f", 0)
        actl(3, "g", 0)
        nt(2, 0)
        nt(2, 1)
        xt(5, 0)
        xqz(4)
        actl(3, "h", 0)
        dd(3, 0)
        actl(3, "f", 0)
        mxl(3, "g", 1)
        mxl(3, "h", 1)
        ee(3, 0)
        ncp(2, 0, "S")
        mxl(3, "f", 1)
        mxp(3, 0)
        ncp(2, 1, "S")
        nn(3, 0)
        xcp(5, 0, "S")
        actl(3, "g", 1)
        yy(2)
        actl(3, "h", 1)
        store(out_1, "nht", 2, None)
        store(out_0, "y", 2, None)
        mxp(3, 1)
        dd(3, 1)
        xt(5, 1)
        actl(3, "f", 1)
        xcp(5, 1, "S")
        xt(5, 2)
        pbias(3, 0)
        ee(3, 1)
        xt(5, 3)
        pbias(3, 1)
        xcp(5, 2, "S")
        nn(3, 1)
        xcp(5, 3, "S")
        mxl(4, "g", 0)
        mxl(4, "h", 0)
        mxl(4, "f", 0)
        actl(4, "g", 0)
        nt(3, 0)
        nt(3, 1)
        xt(6, 0)
        xqz(5)
        actl(4, "h", 0)
        dd(4, 0)
        actl(4, "f", 0)
        mxl(4, "g", 1)
        mxl(4, "h", 1)
        ee(4, 0)
        ncp(3, 0, "S")
        mxl(4, "f", 1)
        mxp(4, 0)
        ncp(3, 1, "S")
        nn(4, 0)
        xcp(6, 0, "S")
        actl(4, "g", 1)
        yy(3)
        actl(4, "h", 1)
        store(out_1, "nht", 3, None)
        store(out_0, "y", 3, None)
        mxp(4, 1)
        dd(4, 1)
        xt(6, 1)
        actl(4, "f", 1)
        xcp(6, 1, "S")
        xt(6, 2)
        pbias(4, 0)
        ee(4, 1)
        xt(6, 3)
        pbias(4, 1)
        xcp(6, 2, "S")
        nn(4, 1)
        xcp(6, 3, "S")
        mxl(5, "g", 0)
        mxl(5, "h", 0)
        mxl(5, "f", 0)
        actl(5, "g", 0)
        nt(4, 0)
        nt(4, 1)
        xt(7, 0)
        xqz(6)
        actl(5, "h", 0)
        dd(5, 0)
        actl(5, "f", 0)
        mxl(5, "g", 1)
        mxl(5, "h", 1)
        ee(5, 0)
        ncp(4, 0, "S")
        mxl(5, "f", 1)
        mxp(5, 0)
        ncp(4, 1, "S")
        nn(5, 0)
        xcp(7, 0, "S")
        actl(5, "g", 1)
        yy(4)
        actl(5, "h", 1)
        store(out_1, "nht", 4, None)
        store(out_0, "y", 4, None)
        mxp(5, 1)
        dd(5, 1)
        xt(7, 1)
        actl(5, "f", 1)
        xcp(7, 1, "S")
        xt(7, 2)
        pbias(5, 0)
        ee(5, 1)
        xt(7, 3)
        pbias(5, 1)
        xcp(7, 2, "S")
        nn(5, 1)
        xcp(7, 3, "S")
        mxl(6, "g", 0)
        mxl(6, "h", 0)
        mxl(6, "f", 0)
        actl(6, "g", 0)
        nt(5, 0)
        nt(5, 1)
        xqz(7)
        actl(6, "h", 0)
        dd(6, 0)
        actl(6, "f", 0)
        mxl(6, "g", 1)
        mxl(6, "h", 1)
        ee(6, 0)
        ncp(5, 0, "S")
        mxl(6, "f", 1)
        mxp(6, 0)
        ncp(5, 1, "S")
        nn(6, 0)
        actl(6, "g", 1)
        yy(5)
        actl(6, "h", 1)
        store(out_1, "nht", 5, None)
        store(out_0, "y", 5, None)
        mxp(6, 1)
        dd(6, 1)
        actl(6, "f", 1)
        pbias(6, 0)
        ee(6, 1)
        pbias(6, 1)
        nn(6, 1)
        mxl(7, "h", 0)
        mxl(7, "g", 0)
        mxl(7, "f", 0)
        actl(7, "h", 0)
        nt(6, 0)
        nt(6, 1)
        mxl(7, "g", 1)
        actl(7, "g", 0)
        actl(7, "f", 0)
        ncp(6, 1, "S")
        dd(7, 0)
        mxl(7, "h", 1)
        actl(7, "g", 1)
        ncp(6, 0, "V")
        mxl(7, "f", 1)
        actl(7, "h", 1)
        ee(7, 0)
        yy(6)
        actf2(7, 2)
        dd(7, 1)
        nn(7, 0)
        mxp(7, 0)
        actf2(7, 3)
        ee2(7, 2)
        ee2(7, 3)
        mxp(7, 1)
        nn2(7, 2)
        nt(7, 0)
        nn2(7, 3)
        store(out_1, "nht", 6, None)
        store(out_0, "y", 6, None)
        pbias(7, 0)
        nt(7, 1)
        ncp(7, 0, "S")
        ncp(7, 1, "S")
        pbias(7, 1)
        yh(7, 0)
        store(out_1, "nht", 7, 0)
        store(out_1, "nht", 7, 1)
        store(out_0, "y", 7, 0)
        yh(7, 1)
        store(out_0, "y", 7, 1)
